import numpy as np
import ml_dtypes


def mxq(x, axis, fmt="e4m3"):
    dtype, down = {"e4m3": (ml_dtypes.float8_e4m3fn, 7), "e5m2": (ml_dtypes.float8_e5m2, 14)}[fmt]
    v = np.moveaxis(np.asarray(x, np.float32).astype(ml_dtypes.bfloat16).astype(np.float64), axis, -1)
    blocks = v.reshape(v.shape[:-1] + (-1, 32))
    amax = np.abs(blocks).max(-1, keepdims=True)
    byte = np.maximum(np.where(amax > 0, np.frexp(amax)[1] - 1 + 127, 0) - down, 1)
    scale = np.exp2(byte - 127.0)
    codes = (blocks / scale).astype(np.float32).astype(dtype).astype(np.float64)
    return np.moveaxis((codes * scale).reshape(v.shape), -1, axis)


WIDE = False


def mx_kscale(k):
    if not WIDE:
        return np.ones(k)
    levels = np.array([10, -10, 5, -5, 0])
    a = np.random.permutation(np.resize(levels, k // 512 * 4)).reshape(k // 512, 4)
    idx = np.arange(k)
    return np.exp2(a[idx // 512, idx % 128 // 32])


BF16 = ml_dtypes.bfloat16


def bf(x):
    return np.asarray(x, np.float32).astype(BF16)


def f64(x):
    return np.asarray(x).astype(np.float64)


B, U, F = 16384, 256, 512


def sigmoid(v):
    return 1.0 / (1.0 + np.exp(-v))


def setup_inputs():
    r = np.exp2(np.round(np.log2(mx_kscale(F)) / 2))
    x = np.random.standard_normal((B, F)) * r
    shift = (np.random.standard_normal((U, F)) * r).reshape(U * F)
    semi_axis = np.sqrt(40.0 * F) * (0.1 + 0.4 * np.random.random_sample((U, F))) * r
    sharpness = np.sqrt(F) * (0.5 + 0.5 * np.random.random_sample(U))
    multiplier = np.where(np.random.random_sample(U) > 0.5, 1.0, -1.0) * (1.0 + 0.1 * np.random.standard_normal(U))
    return {"x": bf(x), "shift": bf(shift), "semi_axis": bf(semi_axis), "sharpness": bf(sharpness), "multiplier": bf(multiplier)}


def reference(x, shift, semi_axis, sharpness, multiplier):
    x = f64(x)
    semi_axis = f64(semi_axis)
    u, f = semi_axis.shape
    s = f64(shift).reshape(u, f)
    inv = 1.0 / np.square(semi_axis)
    quad = ((mxq(np.square(x), 1, "e4m3") @ mxq(inv, 1, "e4m3").T)
            + 2.0 * (mxq(x, 1, "e4m3") @ mxq(s * inv, 1, "e4m3").T)
            + np.sum(np.square(s) * inv, axis=1))
    ellipsoidal = 1.0 - quad
    return sigmoid(ellipsoidal * f64(sharpness)) * f64(multiplier)

@@ -1,0 +1,295 @@
+from contextlib import ExitStack
+
+import concourse.mybir as mybir
+from concourse.masks import make_identity
+
+F32 = mybir.dt.float32
+BF16 = mybir.dt.bfloat16
+U32 = mybir.dt.uint32
+U8 = mybir.dt.uint8
+FP8X4 = mybir.dt.float8_e4m3fn_x4
+ACT = mybir.ActivationFunctionType
+ALU = mybir.AluOpType
+
+P = 128
+B, U, F = 16384, 256, 512
+FLOPS = 2 * 2 * B * U * F
+
+ROW_TILES = B // P
+CHUNK_TILES = 4
+N_CHUNKS = ROW_TILES // CHUNK_TILES
+LOAD_TILES = [4, 4] + [8] * 15
+X_BUFS = 8
+MANUAL = False
+
+
+def vector_square_columns(c):
+    if c < 3:
+        return 0
+    return 1216
+
+
+def tile_boundedparaboloids_t_kernel(tc, x, shift, semi_axis, sharpness, multiplier, out):
+    nc = tc.nc
+    assert sum(LOAD_TILES) == ROW_TILES
+    with ExitStack() as ctx:
+        const = ctx.enter_context(tc.tile_pool(name="const", bufs=1))
+        xpool = ctx.enter_context(tc.tile_pool(name="xpool", bufs=X_BUFS))
+        ggpool = ctx.enter_context(tc.tile_pool(name="ggpool", bufs=4))
+        cpool = ctx.enter_context(tc.tile_pool(name="cpool", bufs=4))
+        spool = ctx.enter_context(tc.tile_pool(name="spool", bufs=3))
+        opool = ctx.enter_context(tc.tile_pool(name="opool", bufs=4))
+        ps_x = ctx.enter_context(tc.psum_pool(name="ps_x", bufs=2))
+        ps_q = ctx.enter_context(tc.psum_pool(name="ps_q", bufs=4))
+        ps_o = ctx.enter_context(tc.psum_pool(name="ps_o", bufs=2))
+        if MANUAL:
+            ctx.enter_context(tc.manual_schedule())
+
+        load_base = []
+        chunk_home = []
+        base = 0
+        for j, t_count in enumerate(LOAD_TILES):
+            load_base.append(base)
+            for t0 in range(0, t_count, CHUNK_TILES):
+                chunk_home.append((j, t0))
+            base += t_count * P
+        last_chunk_of_load = {}
+        for c, (j, t0) in enumerate(chunk_home):
+            last_chunk_of_load[j] = c
+
+        x_tiles = {}
+
+        def load_x(j):
+            if j >= len(LOAD_TILES):
+                return
+            t_count = LOAD_TILES[j]
+            xt = xpool.tile([P, 8 * F], BF16, name="x_sb", tag="x_sb")
+            rows = x[load_base[j] : load_base[j] + t_count * P, :]
+            nc.sync.dma_start(out=xt[:, 0 : t_count * F], in_=rows.rearrange("(p t) f -> p (t f)", t=t_count))
+            x_tiles[j] = xt
+
+        semi_sb = const.tile([P, 2, F], BF16, name="semi_sb")
+        nc.sync.dma_start(out=semi_sb[:], in_=semi_axis.rearrange("(h p) f -> p h f", p=P))
+        shift_sb = const.tile([P, 2, F], BF16, name="shift_sb")
+        nc.sync.dma_start(out=shift_sb[:], in_=shift.rearrange("(h p f) -> p h f", h=2, p=P))
+        load_x(0)
+        load_x(1)
+        rows_bf = const.tile([P, P + U], BF16, name="rows_bf")
+        nc.vector.memset(rows_bf[:], 0.0)
+        nc.sync.dma_start(out=rows_bf[0:2, 0:P], in_=sharpness.rearrange("(h p) -> h p", h=2))
+        nc.sync.dma_start(out=rows_bf[0:1, P : P + U], in_=multiplier.rearrange("(o u) -> o u", o=1))
+        for j in range(2, X_BUFS):
+            load_x(j)
+
+        ident = const.tile([P, P], F32, name="ident")
+        make_identity(nc, ident[:])
+        ones_bf = const.tile([P, P], BF16, name="ones_bf")
+        nc.vector.memset(ones_bf[:], 1.0)
+        warm = const.tile([P, 1], F32, name="warm")
+        nc.vector.memset(warm[:], 0.0)
+        warm_out = const.tile([P, 1], F32, name="warm_out")
+        nc.scalar.activation(out=warm_out[:], in_=warm[:], func=ACT.Sigmoid)
+
+        semi_sq = const.tile([P, 2, F], F32, name="semi_sq")
+        inv = const.tile([P, 2, F], F32, name="inv")
+        shift2 = const.tile([P, 2, F], BF16, name="shift2")
+        shift_sq = const.tile([P, 2, F], F32, name="shift_sq")
+        c_terms = const.tile([P, 2, F], F32, name="c_terms")
+        c_junk = const.tile([P, F], F32, name="c_junk")
+        c_sum = const.tile([P, 2], F32, name="c_sum")
+        w_bf = const.tile([P, 4 * F], BF16, name="w_bf")
+        w_grouped = const.tile([P, 4 * F], BF16, name="w_grouped", align_bytes=64)
+        w_codes = const.tile([P, F], U32, name="w_codes", align_bytes=64)
+        w_scales = const.tile([P, F], U8, name="w_scales", align_bytes=64)
+        rows_f32 = const.tile([P, P], F32, name="rows_f32")
+        neg_sharp = const.tile([P, 2], F32, name="neg_sharp")
+        bias = const.tile([P, 2], F32, name="bias")
+        mult_all = const.tile([P, 2 * U], F32, name="mult_all")
+
+        def weights_start():
+            nc.gpsimd.tensor_scalar(out=shift2[:], in0=shift_sb[:], scalar1=2.0, scalar2=0.0, op0=ALU.mult, op1=ALU.add)
+            nc.gpsimd.tensor_tensor(out=shift_sq[:], in0=shift_sb[:], in1=shift_sb[:], op=ALU.mult)
+            nc.gpsimd.tensor_scalar(out=rows_f32[:], in0=rows_bf[:, 0:P], scalar1=1.0, scalar2=0.0, op0=ALU.mult, op1=ALU.add)
+            for h in range(2):
+                nc.scalar.activation(out=semi_sq[:, h, :], in_=semi_sb[:, h, :], func=ACT.Square)
+            for h in range(2):
+                nc.vector.reciprocal(out=inv[:, h, :], in_=semi_sq[:, h, :])
+
+        def weights_round(h):
+            nc.scalar.copy(out=w_bf[:, h * F : (h + 1) * F], in_=inv[:, h, :])
+            nc.gpsimd.tensor_tensor(out=w_bf[:, (2 + h) * F : (3 + h) * F], in0=shift2[:, h, :], in1=inv[:, h, :], op=ALU.mult)
+            nc.gpsimd.tensor_tensor(out=c_terms[:, h, :], in0=shift_sq[:, h, :], in1=inv[:, h, :], op=ALU.mult)
+
+        def small_vectors_tensor():
+            sharp_ps = ps_q.tile([P, F], F32, name="sharp_ps", tag="q")
+            nc.tensor.transpose(sharp_ps[:, 0:P], rows_f32[:], ident[:])
+            nc.vector.tensor_scalar(out=neg_sharp[:], in0=sharp_ps[:, 0:2], scalar1=-1.0, scalar2=None, op0=ALU.mult)
+            mult_ps = ps_q.tile([P, F], F32, name="mult_ps", tag="q")
+            nc.tensor.matmul(out=mult_ps[:, 0:U], lhsT=ones_bf[:], rhs=rows_bf[:, P : P + U], start=True, stop=True)
+            for r in range(2):
+                nc.vector.tensor_copy(out=mult_all[:, r * U : (r + 1) * U], in_=mult_ps[:, 0:U])
+
+        def weights_finish():
+            w_words = w_bf[:].bitcast(F32)
+            g_words = w_grouped[:].bitcast(F32)
+            for m in range(2):
+                wt = ps_q.tile([P, 2, U], F32, name="wt", tag="q")
+                for h in range(2):
+                    for u in range(2):
+                        col = 512 * m + 256 * h + P * u
+                        nc.tensor.transpose(wt[:, u, h * P : (h + 1) * P], w_words[:, col : col + P], ident[:])
+                nc.vector.tensor_copy(
+                    out=g_words[:, 512 * m : 512 * (m + 1)].rearrange("p (c u) -> p c u", u=2),
+                    in_=wt[:].rearrange("p u c -> p c u"),
+                )
+            nc.vector.quantize_mx(out=w_codes[:].bitcast(FP8X4), scales=w_scales[:], in_=w_grouped[:])
+            for h in range(2):
+                nc.scalar.activation(out=c_junk[:], in_=c_terms[:, h, :], func=ACT.Copy, accum_out=c_sum[:, h : h + 1])
+            nc.vector.scalar_tensor_tensor(
+                out=bias[:], in0=c_sum[:], scalar=-1.0, in1=neg_sharp[:], op0=ALU.add, op1=ALU.mult
+            )
+
+        xt_banks = {}
+        gg_tiles = {}
+        code_tiles = {}
+        q_banks = {}
+        sig_tiles = {}
+        ot_banks = {}
+
+        def live(c):
+            return 0 <= c < N_CHUNKS
+
+        def transposes_in(c):
+            if not live(c):
+                return
+            j, t0 = chunk_home[c]
+            words = x_tiles[j][:].bitcast(F32)
+            banks = []
+            for half in range(2):
+                xt = ps_x.tile([P, 2, 2 * P], F32, name="xt", tag="xt")
+                for tt in range(2):
+                    for u in range(2):
+                        col = (t0 + 2 * half + tt) * (F // 2) + P * u
+                        nc.tensor.transpose(xt[:, u, tt * P : (tt + 1) * P], words[:, col : col + P], ident[:])
+                banks.append(xt)
+            xt_banks[c] = banks
+            if last_chunk_of_load[j] == c:
+                load_x(j + X_BUFS)
+
+        def copy_in(c):
+            if not live(c):
+                return
+            gg = ggpool.tile([P, 8 * F], BF16, name="gg", tag="gg", align_bytes=64)
+            gg_words = gg[:].bitcast(F32)
+            for half in range(2):
+                nc.scalar.copy(
+                    out=gg_words[:, 512 * half : 512 * (half + 1)].rearrange("p (c u) -> p c u", u=2),
+                    in_=xt_banks[c][half][:].rearrange("p u c -> p c u"),
+                )
+            gg_tiles[c] = gg
+
+        def square_scalar(c):
+            if not live(c):
+                return
+            sv = vector_square_columns(c)
+            gg = gg_tiles[c]
+            if sv < 4 * F:
+                nc.scalar.activation(out=gg[:, 4 * F + sv : 8 * F], in_=gg[:, sv : 4 * F], func=ACT.Square)
+
+        def square_vector(c):
+            if not live(c):
+                return
+            sv = vector_square_columns(c)
+            gg = gg_tiles[c]
+            if sv > 0:
+                nc.vector.tensor_tensor(out=gg[:, 4 * F : 4 * F + sv], in0=gg[:, 0:sv], in1=gg[:, 0:sv], op=ALU.mult)
+
+        def quantise(c):
+            if not live(c):
+                return
+            codes = cpool.tile([P, 2 * F], U32, name="codes", tag="codes", align_bytes=64)
+            scales = cpool.tile([P, 2 * F], U8, name="scales", tag="scales", align_bytes=64)
+            nc.vector.quantize_mx(out=codes[:].bitcast(FP8X4), scales=scales[:], in_=gg_tiles[c][:])
+            code_tiles[c] = (codes, scales)
+
+        def mx_passes(c):
+            if not live(c):
+                return
+            codes, scales = code_tiles[c]
+            banks = []
+            for h in range(2):
+                q = ps_q.tile([P, F], F32, name="q", tag="q")
+                for m in range(2):
+                    w_cols = slice(U * m + P * h, U * m + P * (h + 1))
+                    x_cols = slice(F * (1 - m), F * (2 - m))
+                    nc.tensor.matmul_mx(
+                        out=q[:],
+                        lhsT=w_codes[:, w_cols].bitcast(FP8X4),
+                        lhsT_scale=w_scales[:, w_cols],
+                        rhs=codes[:, x_cols].bitcast(FP8X4),
+                        rhs_scale=scales[:, x_cols],
+                        start=(m == 0),
+                        stop=(m == 1),
+                    )
+                banks.append(q)
+            q_banks[c] = banks
+
+        def sigmoid(c):
+            if not live(c):
+                return
+            sig = spool.tile([P, 2 * F], F32, name="sig", tag="sig")
+            for h in range(2):
+                nc.scalar.activation(
+                    out=sig[:, h * F : (h + 1) * F],
+                    in_=q_banks[c][h][:],
+                    func=ACT.Sigmoid,
+                    scale=neg_sharp[:, h : h + 1],
+                    bias=bias[:, h : h + 1],
+                )
+            sig_tiles[c] = sig
+
+        def transposes_out(c):
+            if not live(c):
+                return
+            sig = sig_tiles[c]
+            banks = []
+            for half in range(2):
+                ot = ps_o.tile([P, 2 * U], F32, name="ot", tag="ot")
+                for tt in range(2):
+                    for h in range(2):
+                        col = h * F + (2 * half + tt) * P
+                        nc.tensor.transpose(ot[:, tt * U + h * P : tt * U + (h + 1) * P], sig[:, col : col + P], ident[:])
+                banks.append(ot)
+            ot_banks[c] = banks
+
+        def finish(c):
+            if not live(c):
+                return
+            j, t0 = chunk_home[c]
+            t_count = LOAD_TILES[j]
+            res = opool.tile([P, CHUNK_TILES * U], F32, name="res", tag="res")
+            for half in range(2):
+                nc.vector.tensor_tensor(
+                    out=res[:, half * 2 * U : (half + 1) * 2 * U], in0=ot_banks[c][half][:], in1=mult_all[:], op=ALU.mult
+                )
+            rows = out[load_base[j] : load_base[j] + t_count * P, :].rearrange("(p t) u -> p (t u)", t=t_count)
+            nc.sync.dma_start(out=rows[:, t0 * U : (t0 + CHUNK_TILES) * U], in_=res[:])
+
+        weights_start()
+        for i in range(-3, N_CHUNKS + 1):
+            copy_in(i + 2)
+            quantise(i + 1)
+            if i == 0:
+                weights_finish()
+            mx_passes(i)
+            square_scalar(i + 2)
+            square_vector(i + 2)
+            if i == -2:
+                weights_round(0)
+            if i == -1:
+                weights_round(1)
+                small_vectors_tensor()
+            sigmoid(i)
+            transposes_out(i - 1)
+            finish(i - 1)
+            transposes_in(i + 3)

@@ -20,7 +20,7 @@ CHUNK_TILES = 4
 N_CHUNKS = ROW_TILES // CHUNK_TILES
 LOAD_TILES = [4, 4] + [8] * 15
 X_BUFS = 8
-MANUAL = False
+MANUAL = True
 
 
 def vector_square_columns(c):

@@ -20,13 +20,13 @@ CHUNK_TILES = 4
 N_CHUNKS = ROW_TILES // CHUNK_TILES
 LOAD_TILES = [4, 4] + [8] * 15
 X_BUFS = 8
-MANUAL = True
+MANUAL = False
 
 
 def vector_square_columns(c):
     if c < 3:
         return 0
-    return 1216
+    return 1536
 
 
 def tile_boundedparaboloids_t_kernel(tc, x, shift, semi_axis, sharpness, multiplier, out):

@@ -20,13 +20,9 @@ CHUNK_TILES = 4
 N_CHUNKS = ROW_TILES // CHUNK_TILES
 LOAD_TILES = [4, 4] + [8] * 15
 X_BUFS = 8
-MANUAL = False
-
-
-def vector_square_columns(c):
-    if c < 3:
-        return 0
-    return 1536
+MANUAL = True
+SCALAR_SQUARE_CHUNKS = 3
+OUT_LAG = 2
 
 
 def tile_boundedparaboloids_t_kernel(tc, x, shift, semi_axis, sharpness, multiplier, out):
@@ -37,7 +33,7 @@ def tile_boundedparaboloids_t_kernel(tc, x, shift, semi_axis, sharpness, multipl
         xpool = ctx.enter_context(tc.tile_pool(name="xpool", bufs=X_BUFS))
         ggpool = ctx.enter_context(tc.tile_pool(name="ggpool", bufs=4))
         cpool = ctx.enter_context(tc.tile_pool(name="cpool", bufs=4))
-        spool = ctx.enter_context(tc.tile_pool(name="spool", bufs=3))
+        spool = ctx.enter_context(tc.tile_pool(name="spool", bufs=4))
         opool = ctx.enter_context(tc.tile_pool(name="opool", bufs=4))
         ps_x = ctx.enter_context(tc.psum_pool(name="ps_x", bufs=2))
         ps_q = ctx.enter_context(tc.psum_pool(name="ps_q", bufs=4))
@@ -77,6 +73,7 @@ def tile_boundedparaboloids_t_kernel(tc, x, shift, semi_axis, sharpness, multipl
         rows_bf = const.tile([P, P + U], BF16, name="rows_bf")
         nc.vector.memset(rows_bf[:], 0.0)
         nc.sync.dma_start(out=rows_bf[0:2, 0:P], in_=sharpness.rearrange("(h p) -> h p", h=2))
+        nc.sync.dma_start(out=rows_bf[2:4, 0:P], in_=multiplier.rearrange("(h p) -> h p", h=2))
         nc.sync.dma_start(out=rows_bf[0:1, P : P + U], in_=multiplier.rearrange("(o u) -> o u", o=1))
         for j in range(2, X_BUFS):
             load_x(j)
@@ -104,7 +101,8 @@ def tile_boundedparaboloids_t_kernel(tc, x, shift, semi_axis, sharpness, multipl
         rows_f32 = const.tile([P, P], F32, name="rows_f32")
         neg_sharp = const.tile([P, 2], F32, name="neg_sharp")
         bias = const.tile([P, 2], F32, name="bias")
-        mult_all = const.tile([P, 2 * U], F32, name="mult_all")
+        mult_col = const.tile([P, 1], F32, name="mult_col")
+        mult_rep = const.tile([P, CHUNK_TILES, P], F32, name="mult_rep")
 
         def weights_start():
             nc.gpsimd.tensor_scalar(out=shift2[:], in0=shift_sb[:], scalar1=2.0, scalar2=0.0, op0=ALU.mult, op1=ALU.add)
@@ -120,16 +118,16 @@ def tile_boundedparaboloids_t_kernel(tc, x, shift, semi_axis, sharpness, multipl
             nc.gpsimd.tensor_tensor(out=w_bf[:, (2 + h) * F : (3 + h) * F], in0=shift2[:, h, :], in1=inv[:, h, :], op=ALU.mult)
             nc.gpsimd.tensor_tensor(out=c_terms[:, h, :], in0=shift_sq[:, h, :], in1=inv[:, h, :], op=ALU.mult)
 
-        def small_vectors_tensor():
-            sharp_ps = ps_q.tile([P, F], F32, name="sharp_ps", tag="q")
-            nc.tensor.transpose(sharp_ps[:, 0:P], rows_f32[:], ident[:])
-            nc.vector.tensor_scalar(out=neg_sharp[:], in0=sharp_ps[:, 0:2], scalar1=-1.0, scalar2=None, op0=ALU.mult)
+        def small_vectors():
+            cols_ps = ps_q.tile([P, F], F32, name="cols_ps", tag="q")
+            nc.tensor.transpose(cols_ps[:, 0:P], rows_f32[:], ident[:])
+            nc.vector.tensor_scalar(out=neg_sharp[:], in0=cols_ps[:, 0:2], scalar1=-1.0, scalar2=None, op0=ALU.mult)
+            nc.vector.tensor_copy(out=mult_col[:], in_=cols_ps[:, 3:4])
             mult_ps = ps_q.tile([P, F], F32, name="mult_ps", tag="q")
             nc.tensor.matmul(out=mult_ps[:, 0:U], lhsT=ones_bf[:], rhs=rows_bf[:, P : P + U], start=True, stop=True)
-            for r in range(2):
-                nc.vector.tensor_copy(out=mult_all[:, r * U : (r + 1) * U], in_=mult_ps[:, 0:U])
+            nc.vector.tensor_copy(out=mult_rep[:], in_=mult_ps[:, 0:P].unsqueeze(1).to_broadcast([P, CHUNK_TILES, P]))
 
-        def weights_finish():
+        def weights_quantise():
             w_words = w_bf[:].bitcast(F32)
             g_words = w_grouped[:].bitcast(F32)
             for m in range(2):
@@ -143,6 +141,8 @@ def tile_boundedparaboloids_t_kernel(tc, x, shift, semi_axis, sharpness, multipl
                     in_=wt[:].rearrange("p u c -> p c u"),
                 )
             nc.vector.quantize_mx(out=w_codes[:].bitcast(FP8X4), scales=w_scales[:], in_=w_grouped[:])
+
+        def sigmoid_constants():
             for h in range(2):
                 nc.scalar.activation(out=c_junk[:], in_=c_terms[:, h, :], func=ACT.Copy, accum_out=c_sum[:, h : h + 1])
             nc.vector.scalar_tensor_tensor(
@@ -155,6 +155,7 @@ def tile_boundedparaboloids_t_kernel(tc, x, shift, semi_axis, sharpness, multipl
         q_banks = {}
         sig_tiles = {}
         ot_banks = {}
+        res_tiles = {}
 
         def live(c):
             return 0 <= c < N_CHUNKS
@@ -188,21 +189,14 @@ def tile_boundedparaboloids_t_kernel(tc, x, shift, semi_axis, sharpness, multipl
                 )
             gg_tiles[c] = gg
 
-        def square_scalar(c):
+        def square(c):
             if not live(c):
                 return
-            sv = vector_square_columns(c)
             gg = gg_tiles[c]
-            if sv < 4 * F:
-                nc.scalar.activation(out=gg[:, 4 * F + sv : 8 * F], in_=gg[:, sv : 4 * F], func=ACT.Square)
-
-        def square_vector(c):
-            if not live(c):
-                return
-            sv = vector_square_columns(c)
-            gg = gg_tiles[c]
-            if sv > 0:
-                nc.vector.tensor_tensor(out=gg[:, 4 * F : 4 * F + sv], in0=gg[:, 0:sv], in1=gg[:, 0:sv], op=ALU.mult)
+            if c < SCALAR_SQUARE_CHUNKS:
+                nc.scalar.activation(out=gg[:, 4 * F : 8 * F], in_=gg[:, 0 : 4 * F], func=ACT.Square)
+            else:
+                nc.vector.tensor_tensor(out=gg[:, 4 * F : 8 * F], in0=gg[:, 0 : 4 * F], in1=gg[:, 0 : 4 * F], op=ALU.mult)
 
         def quantise(c):
             if not live(c):
@@ -238,7 +232,7 @@ def tile_boundedparaboloids_t_kernel(tc, x, shift, semi_axis, sharpness, multipl
             if not live(c):
                 return
             sig = spool.tile([P, 2 * F], F32, name="sig", tag="sig")
-            for h in range(2):
+            for h in (1, 0):
                 nc.scalar.activation(
                     out=sig[:, h * F : (h + 1) * F],
                     in_=q_banks[c][h][:],
@@ -246,6 +240,9 @@ def tile_boundedparaboloids_t_kernel(tc, x, shift, semi_axis, sharpness, multipl
                     scale=neg_sharp[:, h : h + 1],
                     bias=bias[:, h : h + 1],
                 )
+            nc.gpsimd.tensor_scalar(
+                out=sig[:, F : 2 * F], in0=sig[:, F : 2 * F], scalar1=mult_col[:, 0:1], scalar2=0.0, op0=ALU.mult, op1=ALU.add
+            )
             sig_tiles[c] = sig
 
         def transposes_out(c):
@@ -253,12 +250,11 @@ def tile_boundedparaboloids_t_kernel(tc, x, shift, semi_axis, sharpness, multipl
                 return
             sig = sig_tiles[c]
             banks = []
-            for half in range(2):
-                ot = ps_o.tile([P, 2 * U], F32, name="ot", tag="ot")
-                for tt in range(2):
-                    for h in range(2):
-                        col = h * F + (2 * half + tt) * P
-                        nc.tensor.transpose(ot[:, tt * U + h * P : tt * U + (h + 1) * P], sig[:, col : col + P], ident[:])
+            for h in range(2):
+                ot = ps_o.tile([P, CHUNK_TILES, P], F32, name="ot", tag="ot")
+                for t in range(CHUNK_TILES):
+                    col = h * F + t * P
+                    nc.tensor.transpose(ot[:, t, :], sig[:, col : col + P], ident[:])
                 banks.append(ot)
             ot_banks[c] = banks
 
@@ -267,29 +263,27 @@ def tile_boundedparaboloids_t_kernel(tc, x, shift, semi_axis, sharpness, multipl
                 return
             j, t0 = chunk_home[c]
             t_count = LOAD_TILES[j]
-            res = opool.tile([P, CHUNK_TILES * U], F32, name="res", tag="res")
-            for half in range(2):
-                nc.vector.tensor_tensor(
-                    out=res[:, half * 2 * U : (half + 1) * 2 * U], in0=ot_banks[c][half][:], in1=mult_all[:], op=ALU.mult
-                )
+            res = opool.tile([P, CHUNK_TILES, U], F32, name="res", tag="res")
+            nc.vector.tensor_tensor(out=res[:, :, 0:P], in0=ot_banks[c][0][:], in1=mult_rep[:], op=ALU.mult)
+            nc.scalar.copy(out=res[:, :, P:U], in_=ot_banks[c][1][:])
             rows = out[load_base[j] : load_base[j] + t_count * P, :].rearrange("(p t) u -> p (t u)", t=t_count)
-            nc.sync.dma_start(out=rows[:, t0 * U : (t0 + CHUNK_TILES) * U], in_=res[:])
+            nc.sync.dma_start(out=rows[:, t0 * U : (t0 + CHUNK_TILES) * U], in_=res[:].rearrange("p t u -> p (t u)"))
 
         weights_start()
-        for i in range(-3, N_CHUNKS + 1):
-            copy_in(i + 2)
+        for i in range(-4, N_CHUNKS + OUT_LAG):
+            transposes_out(i - OUT_LAG)
+            copy_in(i + 3)
+            transposes_in(i + 4)
             quantise(i + 1)
-            if i == 0:
-                weights_finish()
-            mx_passes(i)
-            square_scalar(i + 2)
-            square_vector(i + 2)
+            square(i + 2)
             if i == -2:
                 weights_round(0)
             if i == -1:
                 weights_round(1)
-                small_vectors_tensor()
+                small_vectors()
+                weights_quantise()
+            mx_passes(i + 1)
+            if i == 0:
+                sigmoid_constants()
             sigmoid(i)
-            transposes_out(i - 1)
-            finish(i - 1)
-            transposes_in(i + 3)
+            finish(i - OUT_LAG)

@@ -21,7 +21,7 @@ N_CHUNKS = ROW_TILES // CHUNK_TILES
 LOAD_TILES = [4, 4] + [8] * 15
 X_BUFS = 8
 MANUAL = True
-SCALAR_SQUARE_CHUNKS = 3
+SCALAR_SQUARE_CHUNKS = 2
 OUT_LAG = 2
 
 
@@ -66,15 +66,15 @@ def tile_boundedparaboloids_t_kernel(tc, x, shift, semi_axis, sharpness, multipl
 
         semi_sb = const.tile([P, 2, F], BF16, name="semi_sb")
         nc.sync.dma_start(out=semi_sb[:], in_=semi_axis.rearrange("(h p) f -> p h f", p=P))
+        load_x(0)
         shift_sb = const.tile([P, 2, F], BF16, name="shift_sb")
         nc.sync.dma_start(out=shift_sb[:], in_=shift.rearrange("(h p f) -> p h f", h=2, p=P))
-        load_x(0)
         load_x(1)
-        rows_bf = const.tile([P, P + U], BF16, name="rows_bf")
+        rows_bf = const.tile([P, 2 * P + U], BF16, name="rows_bf")
         nc.vector.memset(rows_bf[:], 0.0)
         nc.sync.dma_start(out=rows_bf[0:2, 0:P], in_=sharpness.rearrange("(h p) -> h p", h=2))
-        nc.sync.dma_start(out=rows_bf[2:4, 0:P], in_=multiplier.rearrange("(h p) -> h p", h=2))
-        nc.sync.dma_start(out=rows_bf[0:1, P : P + U], in_=multiplier.rearrange("(o u) -> o u", o=1))
+        nc.sync.dma_start(out=rows_bf[0:2, P : 2 * P], in_=multiplier.rearrange("(h p) -> h p", h=2))
+        nc.sync.dma_start(out=rows_bf[0:1, 2 * P : 2 * P + U], in_=multiplier.rearrange("(o u) -> o u", o=1))
         for j in range(2, X_BUFS):
             load_x(j)
 
@@ -87,7 +87,7 @@ def tile_boundedparaboloids_t_kernel(tc, x, shift, semi_axis, sharpness, multipl
         warm_out = const.tile([P, 1], F32, name="warm_out")
         nc.scalar.activation(out=warm_out[:], in_=warm[:], func=ACT.Sigmoid)
 
-        semi_sq = const.tile([P, 2, F], F32, name="semi_sq")
+        semi_inv = const.tile([P, 2, F], F32, name="semi_inv")
         inv = const.tile([P, 2, F], F32, name="inv")
         shift2 = const.tile([P, 2, F], BF16, name="shift2")
         shift_sq = const.tile([P, 2, F], F32, name="shift_sq")
@@ -98,7 +98,7 @@ def tile_boundedparaboloids_t_kernel(tc, x, shift, semi_axis, sharpness, multipl
         w_grouped = const.tile([P, 4 * F], BF16, name="w_grouped", align_bytes=64)
         w_codes = const.tile([P, F], U32, name="w_codes", align_bytes=64)
         w_scales = const.tile([P, F], U8, name="w_scales", align_bytes=64)
-        rows_f32 = const.tile([P, P], F32, name="rows_f32")
+        rows_f32 = const.tile([P, 2 * P], F32, name="rows_f32")
         neg_sharp = const.tile([P, 2], F32, name="neg_sharp")
         bias = const.tile([P, 2], F32, name="bias")
         mult_col = const.tile([P, 1], F32, name="mult_col")
@@ -107,44 +107,48 @@ def tile_boundedparaboloids_t_kernel(tc, x, shift, semi_axis, sharpness, multipl
         def weights_start():
             nc.gpsimd.tensor_scalar(out=shift2[:], in0=shift_sb[:], scalar1=2.0, scalar2=0.0, op0=ALU.mult, op1=ALU.add)
             nc.gpsimd.tensor_tensor(out=shift_sq[:], in0=shift_sb[:], in1=shift_sb[:], op=ALU.mult)
-            nc.gpsimd.tensor_scalar(out=rows_f32[:], in0=rows_bf[:, 0:P], scalar1=1.0, scalar2=0.0, op0=ALU.mult, op1=ALU.add)
+            nc.gpsimd.tensor_scalar(out=rows_f32[:], in0=rows_bf[:, 0 : 2 * P], scalar1=1.0, scalar2=0.0, op0=ALU.mult, op1=ALU.add)
             for h in range(2):
-                nc.scalar.activation(out=semi_sq[:, h, :], in_=semi_sb[:, h, :], func=ACT.Square)
-            for h in range(2):
-                nc.vector.reciprocal(out=inv[:, h, :], in_=semi_sq[:, h, :])
+                nc.vector.reciprocal(out=semi_inv[:, h, :], in_=semi_sb[:, h, :])
 
         def weights_round(h):
-            nc.scalar.copy(out=w_bf[:, h * F : (h + 1) * F], in_=inv[:, h, :])
-            nc.gpsimd.tensor_tensor(out=w_bf[:, (2 + h) * F : (3 + h) * F], in0=shift2[:, h, :], in1=inv[:, h, :], op=ALU.mult)
+            nc.scalar.activation(out=inv[:, h, :], in_=semi_inv[:, h, :], func=ACT.Square)
+            nc.scalar.activation(out=w_bf[:, 2 * h * F : (2 * h + 1) * F], in_=semi_inv[:, h, :], func=ACT.Square)
+            nc.gpsimd.tensor_tensor(out=w_bf[:, (2 * h + 1) * F : (2 * h + 2) * F], in0=shift2[:, h, :], in1=inv[:, h, :], op=ALU.mult)
             nc.gpsimd.tensor_tensor(out=c_terms[:, h, :], in0=shift_sq[:, h, :], in1=inv[:, h, :], op=ALU.mult)
 
         def small_vectors():
             cols_ps = ps_q.tile([P, F], F32, name="cols_ps", tag="q")
-            nc.tensor.transpose(cols_ps[:, 0:P], rows_f32[:], ident[:])
+            for v in range(2):
+                nc.tensor.transpose(cols_ps[:, v * P : (v + 1) * P], rows_f32[:, v * P : (v + 1) * P], ident[:])
             nc.vector.tensor_scalar(out=neg_sharp[:], in0=cols_ps[:, 0:2], scalar1=-1.0, scalar2=None, op0=ALU.mult)
-            nc.vector.tensor_copy(out=mult_col[:], in_=cols_ps[:, 3:4])
+            nc.vector.tensor_copy(out=mult_col[:], in_=cols_ps[:, P : P + 1])
             mult_ps = ps_q.tile([P, F], F32, name="mult_ps", tag="q")
-            nc.tensor.matmul(out=mult_ps[:, 0:U], lhsT=ones_bf[:], rhs=rows_bf[:, P : P + U], start=True, stop=True)
-            nc.vector.tensor_copy(out=mult_rep[:], in_=mult_ps[:, 0:P].unsqueeze(1).to_broadcast([P, CHUNK_TILES, P]))
+            nc.tensor.matmul(out=mult_ps[:, 0:U], lhsT=ones_bf[:], rhs=rows_bf[:, 2 * P : 2 * P + U], start=True, stop=True)
+            nc.vector.tensor_copy(out=mult_rep[:], in_=mult_ps[:, P:U].unsqueeze(1).to_broadcast([P, CHUNK_TILES, P]))
 
-        def weights_quantise():
+        def weights_quantise(h):
             w_words = w_bf[:].bitcast(F32)
             g_words = w_grouped[:].bitcast(F32)
+            wt = ps_q.tile([P, 2, U], F32, name="wt", tag="q")
             for m in range(2):
-                wt = ps_q.tile([P, 2, U], F32, name="wt", tag="q")
-                for h in range(2):
-                    for u in range(2):
-                        col = 512 * m + 256 * h + P * u
-                        nc.tensor.transpose(wt[:, u, h * P : (h + 1) * P], w_words[:, col : col + P], ident[:])
-                nc.vector.tensor_copy(
-                    out=g_words[:, 512 * m : 512 * (m + 1)].rearrange("p (c u) -> p c u", u=2),
-                    in_=wt[:].rearrange("p u c -> p c u"),
-                )
-            nc.vector.quantize_mx(out=w_codes[:].bitcast(FP8X4), scales=w_scales[:], in_=w_grouped[:])
+                for u in range(2):
+                    col = 512 * h + 256 * m + P * u
+                    nc.tensor.transpose(wt[:, u, m * P : (m + 1) * P], w_words[:, col : col + P], ident[:])
+            nc.vector.tensor_copy(
+                out=g_words[:, 512 * h : 512 * (h + 1)].rearrange("p (c u) -> p c u", u=2),
+                in_=wt[:].rearrange("p u c -> p c u"),
+            )
+            nc.vector.quantize_mx(
+                out=w_codes[:, U * h : U * (h + 1)].bitcast(FP8X4),
+                scales=w_scales[:, U * h : U * (h + 1)],
+                in_=w_grouped[:, 2 * F * h : 2 * F * (h + 1)],
+            )
 
-        def sigmoid_constants():
-            for h in range(2):
-                nc.scalar.activation(out=c_junk[:], in_=c_terms[:, h, :], func=ACT.Copy, accum_out=c_sum[:, h : h + 1])
+        def sum_c(h):
+            nc.scalar.activation(out=c_junk[:], in_=c_terms[:, h, :], func=ACT.Copy, accum_out=c_sum[:, h : h + 1])
+
+        def sigmoid_bias():
             nc.vector.scalar_tensor_tensor(
                 out=bias[:], in0=c_sum[:], scalar=-1.0, in1=neg_sharp[:], op0=ALU.add, op1=ALU.mult
             )
@@ -214,7 +218,7 @@ def tile_boundedparaboloids_t_kernel(tc, x, shift, semi_axis, sharpness, multipl
             for h in range(2):
                 q = ps_q.tile([P, F], F32, name="q", tag="q")
                 for m in range(2):
-                    w_cols = slice(U * m + P * h, U * m + P * (h + 1))
+                    w_cols = slice(U * h + P * m, U * h + P * (m + 1))
                     x_cols = slice(F * (1 - m), F * (2 - m))
                     nc.tensor.matmul_mx(
                         out=q[:],
@@ -232,7 +236,7 @@ def tile_boundedparaboloids_t_kernel(tc, x, shift, semi_axis, sharpness, multipl
             if not live(c):
                 return
             sig = spool.tile([P, 2 * F], F32, name="sig", tag="sig")
-            for h in (1, 0):
+            for h in range(2):
                 nc.scalar.activation(
                     out=sig[:, h * F : (h + 1) * F],
                     in_=q_banks[c][h][:],
@@ -241,7 +245,7 @@ def tile_boundedparaboloids_t_kernel(tc, x, shift, semi_axis, sharpness, multipl
                     bias=bias[:, h : h + 1],
                 )
             nc.gpsimd.tensor_scalar(
-                out=sig[:, F : 2 * F], in0=sig[:, F : 2 * F], scalar1=mult_col[:, 0:1], scalar2=0.0, op0=ALU.mult, op1=ALU.add
+                out=sig[:, 0:F], in0=sig[:, 0:F], scalar1=mult_col[:, 0:1], scalar2=0.0, op0=ALU.mult, op1=ALU.add
             )
             sig_tiles[c] = sig
 
@@ -264,26 +268,32 @@ def tile_boundedparaboloids_t_kernel(tc, x, shift, semi_axis, sharpness, multipl
             j, t0 = chunk_home[c]
             t_count = LOAD_TILES[j]
             res = opool.tile([P, CHUNK_TILES, U], F32, name="res", tag="res")
-            nc.vector.tensor_tensor(out=res[:, :, 0:P], in0=ot_banks[c][0][:], in1=mult_rep[:], op=ALU.mult)
-            nc.scalar.copy(out=res[:, :, P:U], in_=ot_banks[c][1][:])
+            nc.vector.tensor_tensor(out=res[:, :, P:U], in0=ot_banks[c][1][:], in1=mult_rep[:], op=ALU.mult)
+            nc.scalar.copy(out=res[:, :, 0:P], in_=ot_banks[c][0][:])
             rows = out[load_base[j] : load_base[j] + t_count * P, :].rearrange("(p t) u -> p (t u)", t=t_count)
             nc.sync.dma_start(out=rows[:, t0 * U : (t0 + CHUNK_TILES) * U], in_=res[:].rearrange("p t u -> p (t u)"))
 
         weights_start()
         for i in range(-4, N_CHUNKS + OUT_LAG):
             transposes_out(i - OUT_LAG)
+            if i == -1:
+                weights_quantise(0)
             copy_in(i + 3)
             transposes_in(i + 4)
-            quantise(i + 1)
-            square(i + 2)
             if i == -2:
                 weights_round(0)
             if i == -1:
                 weights_round(1)
+            quantise(i + 1)
+            if i == -1:
                 small_vectors()
-                weights_quantise()
-            mx_passes(i + 1)
+                weights_quantise(1)
+                sum_c(0)
             if i == 0:
-                sigmoid_constants()
+                sigmoid_bias()
+            square(i + 2)
+            if i == -1:
+                sum_c(1)
+            mx_passes(i + 1)
             sigmoid(i)
             finish(i - OUT_LAG)

@@ -35,8 +35,8 @@ def tile_boundedparaboloids_t_kernel(tc, x, shift, semi_axis, sharpness, multipl
         cpool = ctx.enter_context(tc.tile_pool(name="cpool", bufs=4))
         spool = ctx.enter_context(tc.tile_pool(name="spool", bufs=4))
         opool = ctx.enter_context(tc.tile_pool(name="opool", bufs=4))
-        ps_x = ctx.enter_context(tc.psum_pool(name="ps_x", bufs=2))
-        ps_q = ctx.enter_context(tc.psum_pool(name="ps_q", bufs=4))
+        ps_x = ctx.enter_context(tc.psum_pool(name="ps_x", bufs=4))
+        ps_q = ctx.enter_context(tc.psum_pool(name="ps_q", bufs=2))
         ps_o = ctx.enter_context(tc.psum_pool(name="ps_o", bufs=2))
         if MANUAL:
             ctx.enter_context(tc.manual_schedule())
@@ -200,7 +200,15 @@ def tile_boundedparaboloids_t_kernel(tc, x, shift, semi_axis, sharpness, multipl
             if c < SCALAR_SQUARE_CHUNKS:
                 nc.scalar.activation(out=gg[:, 4 * F : 8 * F], in_=gg[:, 0 : 4 * F], func=ACT.Square)
             else:
-                nc.vector.tensor_tensor(out=gg[:, 4 * F : 8 * F], in0=gg[:, 0 : 4 * F], in1=gg[:, 0 : 4 * F], op=ALU.mult)
+                for half in range(2):
+                    x_cols = slice(2 * F * half, 2 * F * (half + 1))
+                    sq_cols = slice(4 * F + 2 * F * half, 4 * F + 2 * F * (half + 1))
+                    nc.vector.tensor_tensor(
+                        out=gg[:, sq_cols].rearrange("p (c u e) -> p c u e", u=2, e=2),
+                        in0=xt_banks[c][half][:].bitcast(BF16).rearrange("p u (c e) -> p c u e", e=2),
+                        in1=gg[:, x_cols].rearrange("p (c u e) -> p c u e", u=2, e=2),
+                        op=ALU.mult,
+                    )
 
         def quantise(c):
             if not live(c):
@@ -291,9 +299,9 @@ def tile_boundedparaboloids_t_kernel(tc, x, shift, semi_axis, sharpness, multipl
                 sum_c(0)
             if i == 0:
                 sigmoid_bias()
-            square(i + 2)
             if i == -1:
                 sum_c(1)
-            mx_passes(i + 1)
             sigmoid(i)
+            mx_passes(i + 1)
             finish(i - OUT_LAG)
+            square(i + 3)

@@ -17,17 +17,16 @@ FLOPS = 2 * 2 * B * U * F
 
 ROW_TILES = B // P
 CHUNK_TILES = 4
-N_CHUNKS = ROW_TILES // CHUNK_TILES
-LOAD_TILES = [4, 4] + [8] * 15
+LOADS = [[4], [4]] + [[4, 4]] * 14 + [[4, 2, 2]]
 X_BUFS = 8
-MANUAL = True
-SCALAR_SQUARE_CHUNKS = 2
 OUT_LAG = 2
+TAIL = 2
+SPARE_BANKS = 3
 
 
 def tile_boundedparaboloids_t_kernel(tc, x, shift, semi_axis, sharpness, multiplier, out):
     nc = tc.nc
-    assert sum(LOAD_TILES) == ROW_TILES
+    assert sum(sum(chunks) for chunks in LOADS) == ROW_TILES
     with ExitStack() as ctx:
         const = ctx.enter_context(tc.tile_pool(name="const", bufs=1))
         xpool = ctx.enter_context(tc.tile_pool(name="xpool", bufs=X_BUFS))
@@ -38,35 +37,41 @@ def tile_boundedparaboloids_t_kernel(tc, x, shift, semi_axis, sharpness, multipl
         ps_x = ctx.enter_context(tc.psum_pool(name="ps_x", bufs=4))
         ps_q = ctx.enter_context(tc.psum_pool(name="ps_q", bufs=2))
         ps_o = ctx.enter_context(tc.psum_pool(name="ps_o", bufs=2))
-        if MANUAL:
-            ctx.enter_context(tc.manual_schedule())
+        ctx.enter_context(tc.manual_schedule())
 
         load_base = []
+        load_tiles = []
         chunk_home = []
         base = 0
-        for j, t_count in enumerate(LOAD_TILES):
+        for j, chunks in enumerate(LOADS):
             load_base.append(base)
-            for t0 in range(0, t_count, CHUNK_TILES):
-                chunk_home.append((j, t0))
-            base += t_count * P
+            load_tiles.append(sum(chunks))
+            t0 = 0
+            for n in chunks:
+                chunk_home.append((j, t0, n))
+                t0 += n
+            base += t0 * P
+        n_chunks = len(chunk_home)
         last_chunk_of_load = {}
-        for c, (j, t0) in enumerate(chunk_home):
+        for c, (j, t0, n) in enumerate(chunk_home):
             last_chunk_of_load[j] = c
 
         x_tiles = {}
 
-        def load_x(j):
-            if j >= len(LOAD_TILES):
+        def load_x(j, pieces=1):
+            if j >= len(LOADS):
                 return
-            t_count = LOAD_TILES[j]
+            t_count = load_tiles[j]
             xt = xpool.tile([P, 8 * F], BF16, name="x_sb", tag="x_sb")
-            rows = x[load_base[j] : load_base[j] + t_count * P, :]
-            nc.sync.dma_start(out=xt[:, 0 : t_count * F], in_=rows.rearrange("(p t) f -> p (t f)", t=t_count))
+            rows = x[load_base[j] : load_base[j] + t_count * P, :].rearrange("(p t) f -> p (t f)", t=t_count)
+            width = t_count * F // pieces
+            for i in range(pieces):
+                nc.sync.dma_start(out=xt[:, i * width : (i + 1) * width], in_=rows[:, i * width : (i + 1) * width])
             x_tiles[j] = xt
 
         semi_sb = const.tile([P, 2, F], BF16, name="semi_sb")
         nc.sync.dma_start(out=semi_sb[:], in_=semi_axis.rearrange("(h p) f -> p h f", p=P))
-        load_x(0)
+        load_x(0, pieces=2)
         shift_sb = const.tile([P, 2, F], BF16, name="shift_sb")
         nc.sync.dma_start(out=shift_sb[:], in_=shift.rearrange("(h p f) -> p h f", h=2, p=P))
         load_x(1)
@@ -83,13 +88,15 @@ def tile_boundedparaboloids_t_kernel(tc, x, shift, semi_axis, sharpness, multipl
         ones_bf = const.tile([P, P], BF16, name="ones_bf")
         nc.vector.memset(ones_bf[:], 1.0)
         warm = const.tile([P, 1], F32, name="warm")
-        nc.vector.memset(warm[:], 0.0)
+        nc.vector.memset(warm[:], 1.0)
         warm_out = const.tile([P, 1], F32, name="warm_out")
-        nc.scalar.activation(out=warm_out[:], in_=warm[:], func=ACT.Sigmoid)
+        nc.scalar.activation(out=warm_out[:], in_=warm[:], func=ACT.Abs_reciprocal_sqrt)
 
-        semi_inv = const.tile([P, 2, F], F32, name="semi_inv")
+        neg_semi_sq = const.tile([P, 2, F], F32, name="neg_semi_sq")
+        root = const.tile([P, 2, F], F32, name="root")
+        guess = const.tile([P, 2, F], F32, name="guess")
+        check = const.tile([P, 2, F], F32, name="check")
         inv = const.tile([P, 2, F], F32, name="inv")
-        shift2 = const.tile([P, 2, F], BF16, name="shift2")
         shift_sq = const.tile([P, 2, F], F32, name="shift_sq")
         c_terms = const.tile([P, 2, F], F32, name="c_terms")
         c_junk = const.tile([P, F], F32, name="c_junk")
@@ -102,32 +109,49 @@ def tile_boundedparaboloids_t_kernel(tc, x, shift, semi_axis, sharpness, multipl
         neg_sharp = const.tile([P, 2], F32, name="neg_sharp")
         bias = const.tile([P, 2], F32, name="bias")
         mult_col = const.tile([P, 1], F32, name="mult_col")
-        mult_rep = const.tile([P, CHUNK_TILES, P], F32, name="mult_rep")
+        mult_row = const.tile([P, U], F32, name="mult_row")
 
-        def weights_start():
-            nc.gpsimd.tensor_scalar(out=shift2[:], in0=shift_sb[:], scalar1=2.0, scalar2=0.0, op0=ALU.mult, op1=ALU.add)
-            nc.gpsimd.tensor_tensor(out=shift_sq[:], in0=shift_sb[:], in1=shift_sb[:], op=ALU.mult)
-            nc.gpsimd.tensor_scalar(out=rows_f32[:], in0=rows_bf[:, 0 : 2 * P], scalar1=1.0, scalar2=0.0, op0=ALU.mult, op1=ALU.add)
-            for h in range(2):
-                nc.vector.reciprocal(out=semi_inv[:, h, :], in_=semi_sb[:, h, :])
+        def negative_square(h):
+            nc.vector.scalar_tensor_tensor(
+                out=neg_semi_sq[:, h, :], in0=semi_sb[:, h, :], scalar=-1.0, in1=semi_sb[:, h, :], op0=ALU.mult, op1=ALU.mult
+            )
 
-        def weights_round(h):
-            nc.scalar.activation(out=inv[:, h, :], in_=semi_inv[:, h, :], func=ACT.Square)
-            nc.scalar.activation(out=w_bf[:, 2 * h * F : (2 * h + 1) * F], in_=semi_inv[:, h, :], func=ACT.Square)
-            nc.gpsimd.tensor_tensor(out=w_bf[:, (2 * h + 1) * F : (2 * h + 2) * F], in0=shift2[:, h, :], in1=inv[:, h, :], op=ALU.mult)
-            nc.gpsimd.tensor_tensor(out=c_terms[:, h, :], in0=shift_sq[:, h, :], in1=inv[:, h, :], op=ALU.mult)
+        def inverse_guess(h):
+            nc.scalar.activation(out=root[:, h, :], in_=neg_semi_sq[:, h, :], func=ACT.Abs_reciprocal_sqrt)
+            nc.scalar.activation(out=guess[:, h, :], in_=root[:, h, :], func=ACT.Square)
+
+        def inverse_check(h):
+            nc.vector.tensor_tensor(out=check[:, h, :], in0=neg_semi_sq[:, h, :], in1=guess[:, h, :], op=ALU.mult)
+
+        def inverse(h):
+            nc.vector.scalar_tensor_tensor(
+                out=inv[:, h, :], in0=check[:, h, :], scalar=2.0, in1=guess[:, h, :], op0=ALU.add, op1=ALU.mult
+            )
+
+        def round_inverse(h):
+            nc.scalar.copy(out=w_bf[:, 2 * h * F : (2 * h + 1) * F], in_=inv[:, h, :])
+
+        def shift_weights(h):
+            nc.vector.scalar_tensor_tensor(
+                out=w_bf[:, (2 * h + 1) * F : (2 * h + 2) * F],
+                in0=shift_sb[:, h, :],
+                scalar=2.0,
+                in1=inv[:, h, :],
+                op0=ALU.mult,
+                op1=ALU.mult,
+            )
 
         def small_vectors():
-            cols_ps = ps_q.tile([P, F], F32, name="cols_ps", tag="q")
+            cols_ps = ps_o.tile([P, F], F32, name="cols_ps", tag="ot")
             for v in range(2):
                 nc.tensor.transpose(cols_ps[:, v * P : (v + 1) * P], rows_f32[:, v * P : (v + 1) * P], ident[:])
-            nc.vector.tensor_scalar(out=neg_sharp[:], in0=cols_ps[:, 0:2], scalar1=-1.0, scalar2=None, op0=ALU.mult)
-            nc.vector.tensor_copy(out=mult_col[:], in_=cols_ps[:, P : P + 1])
-            mult_ps = ps_q.tile([P, F], F32, name="mult_ps", tag="q")
+            nc.scalar.activation(out=neg_sharp[:], in_=cols_ps[:, 0:2], func=ACT.Copy, scale=-1.0)
+            nc.scalar.copy(out=mult_col[:], in_=cols_ps[:, P : P + 1])
+            mult_ps = ps_o.tile([P, F], F32, name="mult_ps", tag="ot")
             nc.tensor.matmul(out=mult_ps[:, 0:U], lhsT=ones_bf[:], rhs=rows_bf[:, 2 * P : 2 * P + U], start=True, stop=True)
-            nc.vector.tensor_copy(out=mult_rep[:], in_=mult_ps[:, P:U].unsqueeze(1).to_broadcast([P, CHUNK_TILES, P]))
+            nc.scalar.copy(out=mult_row[:], in_=mult_ps[:, 0:U])
 
-        def weights_quantise(h):
+        def weights_group(h):
             w_words = w_bf[:].bitcast(F32)
             g_words = w_grouped[:].bitcast(F32)
             wt = ps_q.tile([P, 2, U], F32, name="wt", tag="q")
@@ -135,15 +159,21 @@ def tile_boundedparaboloids_t_kernel(tc, x, shift, semi_axis, sharpness, multipl
                 for u in range(2):
                     col = 512 * h + 256 * m + P * u
                     nc.tensor.transpose(wt[:, u, m * P : (m + 1) * P], w_words[:, col : col + P], ident[:])
-            nc.vector.tensor_copy(
+            nc.scalar.copy(
                 out=g_words[:, 512 * h : 512 * (h + 1)].rearrange("p (c u) -> p c u", u=2),
                 in_=wt[:].rearrange("p u c -> p c u"),
             )
+
+        def weights_quantise(h):
             nc.vector.quantize_mx(
                 out=w_codes[:, U * h : U * (h + 1)].bitcast(FP8X4),
                 scales=w_scales[:, U * h : U * (h + 1)],
                 in_=w_grouped[:, 2 * F * h : 2 * F * (h + 1)],
             )
+
+        def c_products(h):
+            nc.scalar.activation(out=shift_sq[:, h, :], in_=shift_sb[:, h, :], func=ACT.Square)
+            nc.gpsimd.tensor_tensor(out=c_terms[:, h, :], in0=shift_sq[:, h, :], in1=inv[:, h, :], op=ALU.mult)
 
         def sum_c(h):
             nc.scalar.activation(out=c_junk[:], in_=c_terms[:, h, :], func=ACT.Copy, accum_out=c_sum[:, h : h + 1])
@@ -159,18 +189,17 @@ def tile_boundedparaboloids_t_kernel(tc, x, shift, semi_axis, sharpness, multipl
         q_banks = {}
         sig_tiles = {}
         ot_banks = {}
-        res_tiles = {}
 
         def live(c):
-            return 0 <= c < N_CHUNKS
+            return 0 <= c < n_chunks
 
         def transposes_in(c):
             if not live(c):
                 return
-            j, t0 = chunk_home[c]
+            j, t0, n = chunk_home[c]
             words = x_tiles[j][:].bitcast(F32)
             banks = []
-            for half in range(2):
+            for half in range(n // 2):
                 xt = ps_x.tile([P, 2, 2 * P], F32, name="xt", tag="xt")
                 for tt in range(2):
                     for u in range(2):
@@ -181,55 +210,63 @@ def tile_boundedparaboloids_t_kernel(tc, x, shift, semi_axis, sharpness, multipl
             if last_chunk_of_load[j] == c:
                 load_x(j + X_BUFS)
 
+        def copy_in_half(c, half):
+            if half == 0:
+                gg_tiles[c] = ggpool.tile([P, 8 * F], BF16, name="gg", tag="gg", align_bytes=64)
+            gg_words = gg_tiles[c][:].bitcast(F32)
+            nc.scalar.copy(
+                out=gg_words[:, 512 * half : 512 * (half + 1)].rearrange("p (c u) -> p c u", u=2),
+                in_=xt_banks[c][half][:].rearrange("p u c -> p c u"),
+            )
+
+        def square_half(c, half):
+            gg = gg_tiles[c]
+            n = chunk_home[c][2]
+            x_cols = slice(2 * F * half, 2 * F * (half + 1))
+            sq_cols = slice(n * F + 2 * F * half, n * F + 2 * F * (half + 1))
+            nc.vector.tensor_tensor(
+                out=gg[:, sq_cols].rearrange("p (c u e) -> p c u e", u=2, e=2),
+                in0=xt_banks[c][half][:].bitcast(BF16).rearrange("p u (c e) -> p c u e", e=2),
+                in1=gg[:, x_cols].rearrange("p (c u e) -> p c u e", u=2, e=2),
+                op=ALU.mult,
+            )
+
         def copy_in(c):
             if not live(c):
                 return
-            gg = ggpool.tile([P, 8 * F], BF16, name="gg", tag="gg", align_bytes=64)
-            gg_words = gg[:].bitcast(F32)
-            for half in range(2):
-                nc.scalar.copy(
-                    out=gg_words[:, 512 * half : 512 * (half + 1)].rearrange("p (c u) -> p c u", u=2),
-                    in_=xt_banks[c][half][:].rearrange("p u c -> p c u"),
-                )
-            gg_tiles[c] = gg
+            for half in range(chunk_home[c][2] // 2):
+                copy_in_half(c, half)
 
         def square(c):
             if not live(c):
                 return
-            gg = gg_tiles[c]
-            if c < SCALAR_SQUARE_CHUNKS:
-                nc.scalar.activation(out=gg[:, 4 * F : 8 * F], in_=gg[:, 0 : 4 * F], func=ACT.Square)
-            else:
-                for half in range(2):
-                    x_cols = slice(2 * F * half, 2 * F * (half + 1))
-                    sq_cols = slice(4 * F + 2 * F * half, 4 * F + 2 * F * (half + 1))
-                    nc.vector.tensor_tensor(
-                        out=gg[:, sq_cols].rearrange("p (c u e) -> p c u e", u=2, e=2),
-                        in0=xt_banks[c][half][:].bitcast(BF16).rearrange("p u (c e) -> p c u e", e=2),
-                        in1=gg[:, x_cols].rearrange("p (c u e) -> p c u e", u=2, e=2),
-                        op=ALU.mult,
-                    )
+            for half in range(chunk_home[c][2] // 2):
+                square_half(c, half)
 
         def quantise(c):
             if not live(c):
                 return
+            n = chunk_home[c][2]
             codes = cpool.tile([P, 2 * F], U32, name="codes", tag="codes", align_bytes=64)
             scales = cpool.tile([P, 2 * F], U8, name="scales", tag="scales", align_bytes=64)
-            nc.vector.quantize_mx(out=codes[:].bitcast(FP8X4), scales=scales[:], in_=gg_tiles[c][:])
+            nc.vector.quantize_mx(
+                out=codes[:, 0 : 2 * n * P].bitcast(FP8X4), scales=scales[:, 0 : 2 * n * P], in_=gg_tiles[c][:, 0 : 2 * n * F]
+            )
             code_tiles[c] = (codes, scales)
 
         def mx_passes(c):
             if not live(c):
                 return
             codes, scales = code_tiles[c]
+            cols = chunk_home[c][2] * P
             banks = []
             for h in range(2):
                 q = ps_q.tile([P, F], F32, name="q", tag="q")
                 for m in range(2):
                     w_cols = slice(U * h + P * m, U * h + P * (m + 1))
-                    x_cols = slice(F * (1 - m), F * (2 - m))
+                    x_cols = slice(cols * (1 - m), cols * (2 - m))
                     nc.tensor.matmul_mx(
-                        out=q[:],
+                        out=q[:, 0:cols],
                         lhsT=w_codes[:, w_cols].bitcast(FP8X4),
                         lhsT_scale=w_scales[:, w_cols],
                         rhs=codes[:, x_cols].bitcast(FP8X4),
@@ -240,67 +277,114 @@ def tile_boundedparaboloids_t_kernel(tc, x, shift, semi_axis, sharpness, multipl
                 banks.append(q)
             q_banks[c] = banks
 
+        def in_tail(c):
+            return c >= n_chunks - TAIL
+
         def sigmoid(c):
             if not live(c):
                 return
-            sig = spool.tile([P, 2 * F], F32, name="sig", tag="sig")
+            cols = chunk_home[c][2] * P
+            sig = spool.tile([P, 2, F], F32, name="sig", tag="sig")
             for h in range(2):
                 nc.scalar.activation(
-                    out=sig[:, h * F : (h + 1) * F],
-                    in_=q_banks[c][h][:],
+                    out=sig[:, h, 0:cols],
+                    in_=q_banks[c][h][:, 0:cols],
                     func=ACT.Sigmoid,
                     scale=neg_sharp[:, h : h + 1],
                     bias=bias[:, h : h + 1],
                 )
-            nc.gpsimd.tensor_scalar(
-                out=sig[:, 0:F], in0=sig[:, 0:F], scalar1=mult_col[:, 0:1], scalar2=0.0, op0=ALU.mult, op1=ALU.add
-            )
+            if not in_tail(c):
+                nc.gpsimd.tensor_scalar(
+                    out=sig[:, 0, :], in0=sig[:, 0, :], scalar1=mult_col[:, 0:1], scalar2=0.0, op0=ALU.mult, op1=ALU.add
+                )
             sig_tiles[c] = sig
 
         def transposes_out(c):
             if not live(c):
                 return
+            n = chunk_home[c][2]
             sig = sig_tiles[c]
             banks = []
             for h in range(2):
-                ot = ps_o.tile([P, CHUNK_TILES, P], F32, name="ot", tag="ot")
-                for t in range(CHUNK_TILES):
-                    col = h * F + t * P
-                    nc.tensor.transpose(ot[:, t, :], sig[:, col : col + P], ident[:])
+                if c >= n_chunks - SPARE_BANKS:
+                    ot = ps_x.tile([P, CHUNK_TILES, P], F32, name="ot_spare", tag="xt")
+                else:
+                    ot = ps_o.tile([P, CHUNK_TILES, P], F32, name="ot", tag="ot")
+                for t in range(n):
+                    nc.tensor.transpose(ot[:, t, :], sig[:, h, t * P : (t + 1) * P], ident[:])
                 banks.append(ot)
             ot_banks[c] = banks
+
+        def multiply_out(c, res, h):
+            n = chunk_home[c][2]
+            units = slice(h * P, (h + 1) * P)
+            nc.vector.tensor_tensor(
+                out=res[:, 0:n, units],
+                in0=ot_banks[c][h][:, 0:n, :],
+                in1=mult_row[:, units].unsqueeze(1).to_broadcast([P, n, P]),
+                op=ALU.mult,
+            )
 
         def finish(c):
             if not live(c):
                 return
-            j, t0 = chunk_home[c]
-            t_count = LOAD_TILES[j]
+            j, t0, n = chunk_home[c]
+            t_count = load_tiles[j]
             res = opool.tile([P, CHUNK_TILES, U], F32, name="res", tag="res")
-            nc.vector.tensor_tensor(out=res[:, :, P:U], in0=ot_banks[c][1][:], in1=mult_rep[:], op=ALU.mult)
-            nc.scalar.copy(out=res[:, :, 0:P], in_=ot_banks[c][0][:])
+            if in_tail(c):
+                multiply_out(c, res, 0)
+            else:
+                nc.scalar.copy(out=res[:, :, 0:P], in_=ot_banks[c][0][:])
+            multiply_out(c, res, 1)
             rows = out[load_base[j] : load_base[j] + t_count * P, :].rearrange("(p t) u -> p (t u)", t=t_count)
-            nc.sync.dma_start(out=rows[:, t0 * U : (t0 + CHUNK_TILES) * U], in_=res[:].rearrange("p t u -> p (t u)"))
+            nc.sync.dma_start(out=rows[:, t0 * U : (t0 + n) * U], in_=res[:, 0:n, :].rearrange("p t u -> p (t u)"))
 
-        weights_start()
-        for i in range(-4, N_CHUNKS + OUT_LAG):
+        nc.gpsimd.tensor_scalar(out=rows_f32[:], in0=rows_bf[:, 0 : 2 * P], scalar1=1.0, scalar2=0.0, op0=ALU.mult, op1=ALU.add)
+        negative_square(0)
+        negative_square(1)
+        inverse_guess(0)
+        transposes_in(0)
+        transposes_in(1)
+        inverse_check(0)
+        copy_in_half(0, 0)
+        square_half(0, 0)
+        inverse(0)
+        copy_in_half(0, 1)
+        square_half(0, 1)
+        inverse_guess(1)
+        shift_weights(0)
+        round_inverse(0)
+        inverse_check(1)
+        copy_in_half(1, 0)
+        square_half(1, 0)
+        inverse(1)
+        copy_in_half(1, 1)
+        square_half(1, 1)
+        weights_group(0)
+        round_inverse(1)
+        shift_weights(1)
+        weights_quantise(0)
+        nc.scalar.activation(out=warm_out[:], in_=warm[:], func=ACT.Sigmoid)
+        quantise(0)
+        weights_group(1)
+        weights_quantise(1)
+        transposes_in(2)
+        c_products(0)
+        c_products(1)
+        small_vectors()
+        mx_passes(0)
+        copy_in(2)
+        transposes_in(3)
+        square(2)
+        sum_c(0)
+        sum_c(1)
+        for i in range(0, n_chunks + OUT_LAG):
             transposes_out(i - OUT_LAG)
-            if i == -1:
-                weights_quantise(0)
             copy_in(i + 3)
             transposes_in(i + 4)
-            if i == -2:
-                weights_round(0)
-            if i == -1:
-                weights_round(1)
             quantise(i + 1)
-            if i == -1:
-                small_vectors()
-                weights_quantise(1)
-                sum_c(0)
             if i == 0:
                 sigmoid_bias()
-            if i == -1:
-                sum_c(1)
             sigmoid(i)
             mx_passes(i + 1)
             finish(i - OUT_LAG)

@@ -99,7 +99,6 @@ def tile_boundedparaboloids_t_kernel(tc, x, shift, semi_axis, sharpness, multipl
         inv = const.tile([P, 2, F], F32, name="inv")
         shift_sq = const.tile([P, 2, F], F32, name="shift_sq")
         c_terms = const.tile([P, 2, F], F32, name="c_terms")
-        c_junk = const.tile([P, F], F32, name="c_junk")
         c_sum = const.tile([P, 2], F32, name="c_sum")
         w_bf = const.tile([P, 4 * F], BF16, name="w_bf")
         w_grouped = const.tile([P, 4 * F], BF16, name="w_grouped", align_bytes=64)
@@ -129,7 +128,9 @@ def tile_boundedparaboloids_t_kernel(tc, x, shift, semi_axis, sharpness, multipl
             )
 
         def round_inverse(h):
-            nc.scalar.copy(out=w_bf[:, 2 * h * F : (2 * h + 1) * F], in_=inv[:, h, :])
+            nc.gpsimd.tensor_scalar(
+                out=w_bf[:, 2 * h * F : (2 * h + 1) * F], in0=inv[:, h, :], scalar1=1.0, scalar2=0.0, op0=ALU.mult, op1=ALU.add
+            )
 
         def shift_weights(h):
             nc.vector.scalar_tensor_tensor(
@@ -171,12 +172,19 @@ def tile_boundedparaboloids_t_kernel(tc, x, shift, semi_axis, sharpness, multipl
                 in_=w_grouped[:, 2 * F * h : 2 * F * (h + 1)],
             )
 
-        def c_products(h):
-            nc.scalar.activation(out=shift_sq[:, h, :], in_=shift_sb[:, h, :], func=ACT.Square)
-            nc.gpsimd.tensor_tensor(out=c_terms[:, h, :], in0=shift_sq[:, h, :], in1=inv[:, h, :], op=ALU.mult)
+        def square_shift(h):
+            nc.gpsimd.tensor_tensor(out=shift_sq[:, h, :], in0=shift_sb[:, h, :], in1=shift_sb[:, h, :], op=ALU.mult)
 
         def sum_c(h):
-            nc.scalar.activation(out=c_junk[:], in_=c_terms[:, h, :], func=ACT.Copy, accum_out=c_sum[:, h : h + 1])
+            nc.vector.scalar_tensor_tensor(
+                out=c_terms[:, h, :],
+                in0=shift_sq[:, h, :],
+                scalar=1.0,
+                in1=inv[:, h, :],
+                op0=ALU.mult,
+                op1=ALU.mult,
+                accum_out=c_sum[:, h : h + 1],
+            )
 
         def sigmoid_bias():
             nc.vector.scalar_tensor_tensor(
@@ -339,9 +347,9 @@ def tile_boundedparaboloids_t_kernel(tc, x, shift, semi_axis, sharpness, multipl
             rows = out[load_base[j] : load_base[j] + t_count * P, :].rearrange("(p t) u -> p (t u)", t=t_count)
             nc.sync.dma_start(out=rows[:, t0 * U : (t0 + n) * U], in_=res[:, 0:n, :].rearrange("p t u -> p (t u)"))
 
-        nc.gpsimd.tensor_scalar(out=rows_f32[:], in0=rows_bf[:, 0 : 2 * P], scalar1=1.0, scalar2=0.0, op0=ALU.mult, op1=ALU.add)
         negative_square(0)
         negative_square(1)
+        square_shift(0)
         inverse_guess(0)
         transposes_in(0)
         transposes_in(1)
@@ -349,42 +357,41 @@ def tile_boundedparaboloids_t_kernel(tc, x, shift, semi_axis, sharpness, multipl
         copy_in_half(0, 0)
         square_half(0, 0)
         inverse(0)
+        round_inverse(0)
+        square_shift(1)
         copy_in_half(0, 1)
         square_half(0, 1)
         inverse_guess(1)
         shift_weights(0)
-        round_inverse(0)
         inverse_check(1)
         copy_in_half(1, 0)
         square_half(1, 0)
         inverse(1)
-        copy_in_half(1, 1)
-        square_half(1, 1)
-        weights_group(0)
         round_inverse(1)
+        nc.gpsimd.tensor_scalar(out=rows_f32[:], in0=rows_bf[:, 0 : 2 * P], scalar1=1.0, scalar2=0.0, op0=ALU.mult, op1=ALU.add)
+        copy_in_half(1, 1)
+        weights_group(0)
+        square_half(1, 1)
         shift_weights(1)
         weights_quantise(0)
+        transposes_in(2)
         nc.scalar.activation(out=warm_out[:], in_=warm[:], func=ACT.Sigmoid)
         quantise(0)
         weights_group(1)
-        weights_quantise(1)
-        transposes_in(2)
-        c_products(0)
-        c_products(1)
         small_vectors()
+        weights_quantise(1)
         mx_passes(0)
+        sum_c(0)
+        sum_c(1)
+        sigmoid_bias()
         copy_in(2)
         transposes_in(3)
         square(2)
-        sum_c(0)
-        sum_c(1)
         for i in range(0, n_chunks + OUT_LAG):
             transposes_out(i - OUT_LAG)
             copy_in(i + 3)
             transposes_in(i + 4)
             quantise(i + 1)
-            if i == 0:
-                sigmoid_bias()
             sigmoid(i)
             mx_passes(i + 1)
             finish(i - OUT_LAG)

@@ -19,6 +19,8 @@ ROW_TILES = B // P
 CHUNK_TILES = 4
 LOADS = [[4], [4]] + [[4, 4]] * 14 + [[4, 2, 2]]
 X_BUFS = 8
+GPSIMD_ROWS = 64
+FIRST_GPSIMD_CHUNK = 2
 OUT_LAG = 2
 TAIL = 2
 SPARE_BANKS = 3
@@ -230,11 +232,17 @@ def tile_boundedparaboloids_t_kernel(tc, x, shift, semi_axis, sharpness, multipl
         def square_half(c, half):
             gg = gg_tiles[c]
             n = chunk_home[c][2]
-            x_cols = slice(2 * F * half, 2 * F * (half + 1))
-            sq_cols = slice(n * F + 2 * F * half, n * F + 2 * F * (half + 1))
+            rows = 2 * P
+            if n == CHUNK_TILES and half == 0 and c >= FIRST_GPSIMD_CHUNK:
+                rows -= GPSIMD_ROWS
+                x_cols = slice(4 * rows, 2 * F)
+                sq_cols = slice(n * F + 4 * rows, n * F + 2 * F)
+                nc.gpsimd.tensor_tensor(out=gg[:, sq_cols], in0=gg[:, x_cols], in1=gg[:, x_cols], op=ALU.mult)
+            x_cols = slice(2 * F * half, 2 * F * half + 4 * rows)
+            sq_cols = slice(n * F + 2 * F * half, n * F + 2 * F * half + 4 * rows)
             nc.vector.tensor_tensor(
                 out=gg[:, sq_cols].rearrange("p (c u e) -> p c u e", u=2, e=2),
-                in0=xt_banks[c][half][:].bitcast(BF16).rearrange("p u (c e) -> p c u e", e=2),
+                in0=xt_banks[c][half][:].bitcast(BF16).rearrange("p u (c e) -> p c u e", e=2)[:, 0:rows],
                 in1=gg[:, x_cols].rearrange("p (c u e) -> p c u e", u=2, e=2),
                 op=ALU.mult,
             )

@@ -23,7 +23,7 @@ GPSIMD_ROWS = 64
 FIRST_GPSIMD_CHUNK = 2
 OUT_LAG = 2
 TAIL = 2
-SPARE_BANKS = 3
+SPARE_CHUNKS = (3, 2)
 
 
 def tile_boundedparaboloids_t_kernel(tc, x, shift, semi_axis, sharpness, multiplier, out):
@@ -71,11 +71,11 @@ def tile_boundedparaboloids_t_kernel(tc, x, shift, semi_axis, sharpness, multipl
                 nc.sync.dma_start(out=xt[:, i * width : (i + 1) * width], in_=rows[:, i * width : (i + 1) * width])
             x_tiles[j] = xt
 
+        shift_sb = const.tile([P, 2, F], BF16, name="shift_sb")
+        nc.sync.dma_start(out=shift_sb[:], in_=shift.rearrange("(h p f) -> p h f", h=2, p=P))
         semi_sb = const.tile([P, 2, F], BF16, name="semi_sb")
         nc.sync.dma_start(out=semi_sb[:], in_=semi_axis.rearrange("(h p) f -> p h f", p=P))
         load_x(0, pieces=2)
-        shift_sb = const.tile([P, 2, F], BF16, name="shift_sb")
-        nc.sync.dma_start(out=shift_sb[:], in_=shift.rearrange("(h p f) -> p h f", h=2, p=P))
         load_x(1)
         rows_bf = const.tile([P, 2 * P + U], BF16, name="rows_bf")
         nc.vector.memset(rows_bf[:], 0.0)
@@ -130,9 +130,7 @@ def tile_boundedparaboloids_t_kernel(tc, x, shift, semi_axis, sharpness, multipl
             )
 
         def round_inverse(h):
-            nc.gpsimd.tensor_scalar(
-                out=w_bf[:, 2 * h * F : (2 * h + 1) * F], in0=inv[:, h, :], scalar1=1.0, scalar2=0.0, op0=ALU.mult, op1=ALU.add
-            )
+            nc.scalar.copy(out=w_bf[:, 2 * h * F : (2 * h + 1) * F], in_=inv[:, h, :])
 
         def shift_weights(h):
             nc.vector.scalar_tensor_tensor(
@@ -175,7 +173,7 @@ def tile_boundedparaboloids_t_kernel(tc, x, shift, semi_axis, sharpness, multipl
             )
 
         def square_shift(h):
-            nc.gpsimd.tensor_tensor(out=shift_sq[:, h, :], in0=shift_sb[:, h, :], in1=shift_sb[:, h, :], op=ALU.mult)
+            nc.scalar.activation(out=shift_sq[:, h, :], in_=shift_sb[:, h, :], func=ACT.Square)
 
         def sum_c(h):
             nc.vector.scalar_tensor_tensor(
@@ -322,7 +320,7 @@ def tile_boundedparaboloids_t_kernel(tc, x, shift, semi_axis, sharpness, multipl
             sig = sig_tiles[c]
             banks = []
             for h in range(2):
-                if c >= n_chunks - SPARE_BANKS:
+                if n_chunks - c in SPARE_CHUNKS:
                     ot = ps_x.tile([P, CHUNK_TILES, P], F32, name="ot_spare", tag="xt")
                 else:
                     ot = ps_o.tile([P, CHUNK_TILES, P], F32, name="ot", tag="ot")
@@ -355,9 +353,11 @@ def tile_boundedparaboloids_t_kernel(tc, x, shift, semi_axis, sharpness, multipl
             rows = out[load_base[j] : load_base[j] + t_count * P, :].rearrange("(p t) u -> p (t u)", t=t_count)
             nc.sync.dma_start(out=rows[:, t0 * U : (t0 + n) * U], in_=res[:, 0:n, :].rearrange("p t u -> p (t u)"))
 
+        square_shift(0)
+        square_shift(1)
         negative_square(0)
         negative_square(1)
-        square_shift(0)
+        nc.gpsimd.tensor_scalar(out=rows_f32[:], in0=rows_bf[:, 0 : 2 * P], scalar1=1.0, scalar2=0.0, op0=ALU.mult, op1=ALU.add)
         inverse_guess(0)
         transposes_in(0)
         transposes_in(1)
@@ -365,30 +365,28 @@ def tile_boundedparaboloids_t_kernel(tc, x, shift, semi_axis, sharpness, multipl
         copy_in_half(0, 0)
         square_half(0, 0)
         inverse(0)
-        round_inverse(0)
-        square_shift(1)
-        copy_in_half(0, 1)
-        square_half(0, 1)
         inverse_guess(1)
-        shift_weights(0)
         inverse_check(1)
+        shift_weights(0)
+        copy_in_half(0, 1)
+        round_inverse(0)
+        square_half(0, 1)
+        inverse(1)
         copy_in_half(1, 0)
         square_half(1, 0)
-        inverse(1)
-        round_inverse(1)
-        nc.gpsimd.tensor_scalar(out=rows_f32[:], in0=rows_bf[:, 0 : 2 * P], scalar1=1.0, scalar2=0.0, op0=ALU.mult, op1=ALU.add)
-        copy_in_half(1, 1)
-        weights_group(0)
-        square_half(1, 1)
         shift_weights(1)
+        weights_group(0)
+        round_inverse(1)
+        copy_in_half(1, 1)
+        quantise(0)
         weights_quantise(0)
         transposes_in(2)
-        nc.scalar.activation(out=warm_out[:], in_=warm[:], func=ACT.Sigmoid)
-        quantise(0)
         weights_group(1)
-        small_vectors()
         weights_quantise(1)
+        nc.scalar.activation(out=warm_out[:], in_=warm[:], func=ACT.Sigmoid)
         mx_passes(0)
+        square_half(1, 1)
+        small_vectors()
         sum_c(0)
         sum_c(1)
         sigmoid_bias()
@@ -396,11 +394,14 @@ def tile_boundedparaboloids_t_kernel(tc, x, shift, semi_axis, sharpness, multipl
         transposes_in(3)
         square(2)
         for i in range(0, n_chunks + OUT_LAG):
-            transposes_out(i - OUT_LAG)
+            if i < n_chunks - 1:
+                transposes_out(i - OUT_LAG)
             copy_in(i + 3)
             transposes_in(i + 4)
             quantise(i + 1)
             sigmoid(i)
+            if i >= n_chunks - 2:
+                transposes_out(i - OUT_LAG + 1)
             mx_passes(i + 1)
             finish(i - OUT_LAG)
             square(i + 3)

@@ -20,10 +20,9 @@ CHUNK_TILES = 4
 LOADS = [[4], [4]] + [[4, 4]] * 14 + [[4, 2, 2]]
 X_BUFS = 8
 GPSIMD_ROWS = 64
-FIRST_GPSIMD_CHUNK = 2
+FIRST_GPSIMD_CHUNK = 5
 OUT_LAG = 2
 TAIL = 2
-SPARE_CHUNKS = (3, 2)
 
 
 def tile_boundedparaboloids_t_kernel(tc, x, shift, semi_axis, sharpness, multiplier, out):
@@ -35,7 +34,7 @@ def tile_boundedparaboloids_t_kernel(tc, x, shift, semi_axis, sharpness, multipl
         ggpool = ctx.enter_context(tc.tile_pool(name="ggpool", bufs=4))
         cpool = ctx.enter_context(tc.tile_pool(name="cpool", bufs=4))
         spool = ctx.enter_context(tc.tile_pool(name="spool", bufs=4))
-        opool = ctx.enter_context(tc.tile_pool(name="opool", bufs=4))
+        opool = ctx.enter_context(tc.tile_pool(name="opool", bufs=6))
         ps_x = ctx.enter_context(tc.psum_pool(name="ps_x", bufs=4))
         ps_q = ctx.enter_context(tc.psum_pool(name="ps_q", bufs=2))
         ps_o = ctx.enter_context(tc.psum_pool(name="ps_o", bufs=2))
@@ -71,10 +70,11 @@ def tile_boundedparaboloids_t_kernel(tc, x, shift, semi_axis, sharpness, multipl
                 nc.sync.dma_start(out=xt[:, i * width : (i + 1) * width], in_=rows[:, i * width : (i + 1) * width])
             x_tiles[j] = xt
 
+        semi_sb = const.tile([P, 2, F], BF16, name="semi_sb")
+        for h in range(2):
+            nc.sync.dma_start(out=semi_sb[:, h, :], in_=semi_axis[h * P : (h + 1) * P, :])
         shift_sb = const.tile([P, 2, F], BF16, name="shift_sb")
         nc.sync.dma_start(out=shift_sb[:], in_=shift.rearrange("(h p f) -> p h f", h=2, p=P))
-        semi_sb = const.tile([P, 2, F], BF16, name="semi_sb")
-        nc.sync.dma_start(out=semi_sb[:], in_=semi_axis.rearrange("(h p) f -> p h f", p=P))
         load_x(0, pieces=2)
         load_x(1)
         rows_bf = const.tile([P, 2 * P + U], BF16, name="rows_bf")
@@ -117,8 +117,10 @@ def tile_boundedparaboloids_t_kernel(tc, x, shift, semi_axis, sharpness, multipl
                 out=neg_semi_sq[:, h, :], in0=semi_sb[:, h, :], scalar=-1.0, in1=semi_sb[:, h, :], op0=ALU.mult, op1=ALU.mult
             )
 
-        def inverse_guess(h):
+        def inverse_root(h):
             nc.scalar.activation(out=root[:, h, :], in_=neg_semi_sq[:, h, :], func=ACT.Abs_reciprocal_sqrt)
+
+        def inverse_guess(h):
             nc.scalar.activation(out=guess[:, h, :], in_=root[:, h, :], func=ACT.Square)
 
         def inverse_check(h):
@@ -173,7 +175,7 @@ def tile_boundedparaboloids_t_kernel(tc, x, shift, semi_axis, sharpness, multipl
             )
 
         def square_shift(h):
-            nc.scalar.activation(out=shift_sq[:, h, :], in_=shift_sb[:, h, :], func=ACT.Square)
+            nc.vector.tensor_tensor(out=shift_sq[:, h, :], in0=shift_sb[:, h, :], in1=shift_sb[:, h, :], op=ALU.mult)
 
         def sum_c(h):
             nc.vector.scalar_tensor_tensor(
@@ -275,7 +277,10 @@ def tile_boundedparaboloids_t_kernel(tc, x, shift, semi_axis, sharpness, multipl
             cols = chunk_home[c][2] * P
             banks = []
             for h in range(2):
-                q = ps_q.tile([P, F], F32, name="q", tag="q")
+                if c == n_chunks - 1:
+                    q = ps_x.tile([P, F], F32, name="q_last", tag="xt")
+                else:
+                    q = ps_q.tile([P, F], F32, name="q", tag="q")
                 for m in range(2):
                     w_cols = slice(U * h + P * m, U * h + P * (m + 1))
                     x_cols = slice(cols * (1 - m), cols * (2 - m))
@@ -320,7 +325,9 @@ def tile_boundedparaboloids_t_kernel(tc, x, shift, semi_axis, sharpness, multipl
             sig = sig_tiles[c]
             banks = []
             for h in range(2):
-                if n_chunks - c in SPARE_CHUNKS:
+                if c == n_chunks - 1:
+                    ot = ps_q.tile([P, CHUNK_TILES, P], F32, name="ot_last", tag="q")
+                elif c == n_chunks - 3:
                     ot = ps_x.tile([P, CHUNK_TILES, P], F32, name="ot_spare", tag="xt")
                 else:
                     ot = ps_o.tile([P, CHUNK_TILES, P], F32, name="ot", tag="ot")
@@ -353,14 +360,16 @@ def tile_boundedparaboloids_t_kernel(tc, x, shift, semi_axis, sharpness, multipl
             rows = out[load_base[j] : load_base[j] + t_count * P, :].rearrange("(p t) u -> p (t u)", t=t_count)
             nc.sync.dma_start(out=rows[:, t0 * U : (t0 + n) * U], in_=res[:, 0:n, :].rearrange("p t u -> p (t u)"))
 
-        square_shift(0)
-        square_shift(1)
         negative_square(0)
         negative_square(1)
+        square_shift(0)
+        square_shift(1)
         nc.gpsimd.tensor_scalar(out=rows_f32[:], in0=rows_bf[:, 0 : 2 * P], scalar1=1.0, scalar2=0.0, op0=ALU.mult, op1=ALU.add)
-        inverse_guess(0)
         transposes_in(0)
         transposes_in(1)
+        inverse_root(0)
+        inverse_root(1)
+        inverse_guess(0)
         inverse_check(0)
         copy_in_half(0, 0)
         square_half(0, 0)
@@ -369,39 +378,56 @@ def tile_boundedparaboloids_t_kernel(tc, x, shift, semi_axis, sharpness, multipl
         inverse_check(1)
         shift_weights(0)
         copy_in_half(0, 1)
-        round_inverse(0)
         square_half(0, 1)
         inverse(1)
-        copy_in_half(1, 0)
-        square_half(1, 0)
-        shift_weights(1)
-        weights_group(0)
-        round_inverse(1)
-        copy_in_half(1, 1)
-        quantise(0)
-        weights_quantise(0)
-        transposes_in(2)
-        weights_group(1)
-        weights_quantise(1)
-        nc.scalar.activation(out=warm_out[:], in_=warm[:], func=ACT.Sigmoid)
-        mx_passes(0)
-        square_half(1, 1)
-        small_vectors()
+        round_inverse(0)
         sum_c(0)
+        nc.scalar.activation(out=warm_out[:], in_=warm[:], func=ACT.Sigmoid)
+        shift_weights(1)
+        round_inverse(1)
+        weights_group(0)
+        quantise(0)
+        copy_in_half(1, 0)
+        weights_group(1)
+        weights_quantise(0)
+        weights_quantise(1)
+        square_half(1, 0)
+        copy_in_half(1, 1)
+        square_half(1, 1)
         sum_c(1)
+        transposes_in(2)
+        small_vectors()
+        mx_passes(0)
         sigmoid_bias()
-        copy_in(2)
+        copy_in_half(2, 0)
+        square_half(2, 0)
+        copy_in_half(2, 1)
+        square_half(2, 1)
         transposes_in(3)
-        square(2)
-        for i in range(0, n_chunks + OUT_LAG):
-            if i < n_chunks - 1:
-                transposes_out(i - OUT_LAG)
+        for i in range(0, n_chunks - 3):
+            transposes_out(i - OUT_LAG)
             copy_in(i + 3)
             transposes_in(i + 4)
             quantise(i + 1)
             sigmoid(i)
-            if i >= n_chunks - 2:
-                transposes_out(i - OUT_LAG + 1)
             mx_passes(i + 1)
             finish(i - OUT_LAG)
             square(i + 3)
+        n = n_chunks
+        transposes_out(n - 5)
+        quantise(n - 2)
+        quantise(n - 1)
+        sigmoid(n - 3)
+        mx_passes(n - 2)
+        finish(n - 5)
+        transposes_out(n - 4)
+        sigmoid(n - 2)
+        mx_passes(n - 1)
+        finish(n - 4)
+        transposes_out(n - 3)
+        sigmoid(n - 1)
+        transposes_out(n - 2)
+        finish(n - 3)
+        transposes_out(n - 1)
+        finish(n - 2)
+        finish(n - 1)

@@ -21,6 +21,7 @@ LOADS = [[4], [4]] + [[4, 4]] * 14 + [[4, 2, 2]]
 X_BUFS = 8
 GPSIMD_ROWS = 64
 FIRST_GPSIMD_CHUNK = 5
+PIECES = 2
 OUT_LAG = 2
 TAIL = 2
 
@@ -73,9 +74,9 @@ def tile_boundedparaboloids_t_kernel(tc, x, shift, semi_axis, sharpness, multipl
         semi_sb = const.tile([P, 2, F], BF16, name="semi_sb")
         for h in range(2):
             nc.sync.dma_start(out=semi_sb[:, h, :], in_=semi_axis[h * P : (h + 1) * P, :])
+        load_x(0, pieces=2)
         shift_sb = const.tile([P, 2, F], BF16, name="shift_sb")
         nc.sync.dma_start(out=shift_sb[:], in_=shift.rearrange("(h p f) -> p h f", h=2, p=P))
-        load_x(0, pieces=2)
         load_x(1)
         rows_bf = const.tile([P, 2 * P + U], BF16, name="rows_bf")
         nc.vector.memset(rows_bf[:], 0.0)
@@ -99,7 +100,7 @@ def tile_boundedparaboloids_t_kernel(tc, x, shift, semi_axis, sharpness, multipl
         guess = const.tile([P, 2, F], F32, name="guess")
         check = const.tile([P, 2, F], F32, name="check")
         inv = const.tile([P, 2, F], F32, name="inv")
-        shift_sq = const.tile([P, 2, F], F32, name="shift_sq")
+        shift_inv = const.tile([P, 2, F], F32, name="shift_inv")
         c_terms = const.tile([P, 2, F], F32, name="c_terms")
         c_sum = const.tile([P, 2], F32, name="c_sum")
         w_bf = const.tile([P, 4 * F], BF16, name="w_bf")
@@ -112,36 +113,37 @@ def tile_boundedparaboloids_t_kernel(tc, x, shift, semi_axis, sharpness, multipl
         mult_col = const.tile([P, 1], F32, name="mult_col")
         mult_row = const.tile([P, U], F32, name="mult_row")
 
-        def negative_square(h):
+        def piece(tile, i):
+            return tile[:, i // PIECES, i % PIECES * (F // PIECES) : (i % PIECES + 1) * (F // PIECES)]
+
+        def negative_square(i):
             nc.vector.scalar_tensor_tensor(
-                out=neg_semi_sq[:, h, :], in0=semi_sb[:, h, :], scalar=-1.0, in1=semi_sb[:, h, :], op0=ALU.mult, op1=ALU.mult
+                out=piece(neg_semi_sq, i), in0=piece(semi_sb, i), scalar=-1.0, in1=piece(semi_sb, i), op0=ALU.mult, op1=ALU.mult
             )
 
-        def inverse_root(h):
-            nc.scalar.activation(out=root[:, h, :], in_=neg_semi_sq[:, h, :], func=ACT.Abs_reciprocal_sqrt)
+        def inverse_root(i):
+            nc.scalar.activation(out=piece(root, i), in_=piece(neg_semi_sq, i), func=ACT.Abs_reciprocal_sqrt)
 
-        def inverse_guess(h):
-            nc.scalar.activation(out=guess[:, h, :], in_=root[:, h, :], func=ACT.Square)
+        def inverse_guess(i):
+            nc.scalar.activation(out=piece(guess, i), in_=piece(root, i), func=ACT.Square)
 
-        def inverse_check(h):
-            nc.vector.tensor_tensor(out=check[:, h, :], in0=neg_semi_sq[:, h, :], in1=guess[:, h, :], op=ALU.mult)
+        def inverse_check(i):
+            nc.vector.tensor_tensor(out=piece(check, i), in0=piece(neg_semi_sq, i), in1=piece(guess, i), op=ALU.mult)
 
-        def inverse(h):
+        def inverse(i):
             nc.vector.scalar_tensor_tensor(
-                out=inv[:, h, :], in0=check[:, h, :], scalar=2.0, in1=guess[:, h, :], op0=ALU.add, op1=ALU.mult
+                out=piece(inv, i), in0=piece(check, i), scalar=2.0, in1=piece(guess, i), op0=ALU.add, op1=ALU.mult
             )
+
+        def shift_times_inverse(h):
+            nc.vector.tensor_tensor(out=shift_inv[:, h, :], in0=shift_sb[:, h, :], in1=inv[:, h, :], op=ALU.mult)
 
         def round_inverse(h):
             nc.scalar.copy(out=w_bf[:, 2 * h * F : (2 * h + 1) * F], in_=inv[:, h, :])
 
-        def shift_weights(h):
-            nc.vector.scalar_tensor_tensor(
-                out=w_bf[:, (2 * h + 1) * F : (2 * h + 2) * F],
-                in0=shift_sb[:, h, :],
-                scalar=2.0,
-                in1=inv[:, h, :],
-                op0=ALU.mult,
-                op1=ALU.mult,
+        def round_shift_inverse(h):
+            nc.scalar.activation(
+                out=w_bf[:, (2 * h + 1) * F : (2 * h + 2) * F], in_=shift_inv[:, h, :], func=ACT.Copy, scale=2.0
             )
 
         def small_vectors():
@@ -174,15 +176,12 @@ def tile_boundedparaboloids_t_kernel(tc, x, shift, semi_axis, sharpness, multipl
                 in_=w_grouped[:, 2 * F * h : 2 * F * (h + 1)],
             )
 
-        def square_shift(h):
-            nc.vector.tensor_tensor(out=shift_sq[:, h, :], in0=shift_sb[:, h, :], in1=shift_sb[:, h, :], op=ALU.mult)
-
         def sum_c(h):
             nc.vector.scalar_tensor_tensor(
                 out=c_terms[:, h, :],
-                in0=shift_sq[:, h, :],
+                in0=shift_inv[:, h, :],
                 scalar=1.0,
-                in1=inv[:, h, :],
+                in1=shift_sb[:, h, :],
                 op0=ALU.mult,
                 op1=ALU.mult,
                 accum_out=c_sum[:, h : h + 1],
@@ -362,49 +361,63 @@ def tile_boundedparaboloids_t_kernel(tc, x, shift, semi_axis, sharpness, multipl
 
         negative_square(0)
         negative_square(1)
-        square_shift(0)
-        square_shift(1)
+        negative_square(2)
+        negative_square(3)
         nc.gpsimd.tensor_scalar(out=rows_f32[:], in0=rows_bf[:, 0 : 2 * P], scalar1=1.0, scalar2=0.0, op0=ALU.mult, op1=ALU.add)
         transposes_in(0)
         transposes_in(1)
         inverse_root(0)
         inverse_root(1)
         inverse_guess(0)
-        inverse_check(0)
-        copy_in_half(0, 0)
-        square_half(0, 0)
-        inverse(0)
         inverse_guess(1)
+        inverse_root(2)
+        inverse_root(3)
+        inverse_guess(2)
+        inverse_guess(3)
+        inverse_check(0)
         inverse_check(1)
-        shift_weights(0)
-        copy_in_half(0, 1)
-        square_half(0, 1)
+        inverse(0)
         inverse(1)
+        inverse_check(2)
+        shift_times_inverse(0)
+        inverse_check(3)
+        inverse(2)
+        inverse(3)
+        copy_in_half(0, 0)
+        copy_in_half(0, 1)
         round_inverse(0)
-        sum_c(0)
-        nc.scalar.activation(out=warm_out[:], in_=warm[:], func=ACT.Sigmoid)
-        shift_weights(1)
+        round_shift_inverse(0)
+        square_half(0, 0)
+        shift_times_inverse(1)
+        square_half(0, 1)
+        copy_in_half(1, 0)
         round_inverse(1)
         weights_group(0)
+        round_shift_inverse(1)
+        sum_c(0)
         quantise(0)
-        copy_in_half(1, 0)
-        weights_group(1)
-        weights_quantise(0)
-        weights_quantise(1)
-        square_half(1, 0)
         copy_in_half(1, 1)
-        square_half(1, 1)
+        nc.scalar.activation(out=warm_out[:], in_=warm[:], func=ACT.Sigmoid)
+        weights_group(1)
+        square_half(1, 0)
+        weights_quantise(0)
         sum_c(1)
+        square_half(1, 1)
+        weights_quantise(1)
         transposes_in(2)
         small_vectors()
         mx_passes(0)
-        sigmoid_bias()
-        copy_in_half(2, 0)
-        square_half(2, 0)
-        copy_in_half(2, 1)
-        square_half(2, 1)
         transposes_in(3)
-        for i in range(0, n_chunks - 3):
+        copy_in(2)
+        sigmoid_bias()
+        quantise(1)
+        square(2)
+        sigmoid(0)
+        copy_in(3)
+        transposes_in(4)
+        mx_passes(1)
+        square(3)
+        for i in range(1, n_chunks - 3):
             transposes_out(i - OUT_LAG)
             copy_in(i + 3)
             transposes_in(i + 4)

@@ -18,7 +18,8 @@ FLOPS = 2 * 2 * B * U * F
 ROW_TILES = B // P
 CHUNK_TILES = 4
 LOADS = [[4], [4]] + [[4, 4]] * 14 + [[4, 2, 2]]
-X_BUFS = 8
+X_BUFS = 5
+O_BUFS = 26
 GPSIMD_ROWS = 64
 FIRST_GPSIMD_CHUNK = 5
 PIECES = 2
@@ -35,7 +36,7 @@ def tile_boundedparaboloids_t_kernel(tc, x, shift, semi_axis, sharpness, multipl
         ggpool = ctx.enter_context(tc.tile_pool(name="ggpool", bufs=4))
         cpool = ctx.enter_context(tc.tile_pool(name="cpool", bufs=4))
         spool = ctx.enter_context(tc.tile_pool(name="spool", bufs=4))
-        opool = ctx.enter_context(tc.tile_pool(name="opool", bufs=6))
+        opool = ctx.enter_context(tc.tile_pool(name="opool", bufs=O_BUFS))
         ps_x = ctx.enter_context(tc.psum_pool(name="ps_x", bufs=4))
         ps_q = ctx.enter_context(tc.psum_pool(name="ps_q", bufs=2))
         ps_o = ctx.enter_context(tc.psum_pool(name="ps_o", bufs=2))
@@ -95,13 +96,13 @@ def tile_boundedparaboloids_t_kernel(tc, x, shift, semi_axis, sharpness, multipl
         warm_out = const.tile([P, 1], F32, name="warm_out")
         nc.scalar.activation(out=warm_out[:], in_=warm[:], func=ACT.Abs_reciprocal_sqrt)
 
-        neg_semi_sq = const.tile([P, 2, F], F32, name="neg_semi_sq")
-        root = const.tile([P, 2, F], F32, name="root")
-        guess = const.tile([P, 2, F], F32, name="guess")
-        check = const.tile([P, 2, F], F32, name="check")
-        inv = const.tile([P, 2, F], F32, name="inv")
-        shift_inv = const.tile([P, 2, F], F32, name="shift_inv")
-        c_terms = const.tile([P, 2, F], F32, name="c_terms")
+        neg_semi_sq = opool.tile([P, 2, F], F32, name="neg_semi_sq", tag="res")
+        root = opool.tile([P, 2, F], F32, name="root", tag="res")
+        guess = opool.tile([P, 2, F], F32, name="guess", tag="res")
+        check = opool.tile([P, 2, F], F32, name="check", tag="res")
+        inv = opool.tile([P, 2, F], F32, name="inv", tag="res")
+        shift_inv = opool.tile([P, 2, F], F32, name="shift_inv", tag="res")
+        c_terms = opool.tile([P, 2, F], F32, name="c_terms", tag="res")
         c_sum = const.tile([P, 2], F32, name="c_sum")
         w_bf = const.tile([P, 4 * F], BF16, name="w_bf")
         w_grouped = const.tile([P, 4 * F], BF16, name="w_grouped", align_bytes=64)
@@ -424,8 +425,8 @@ def tile_boundedparaboloids_t_kernel(tc, x, shift, semi_axis, sharpness, multipl
             quantise(i + 1)
             sigmoid(i)
             mx_passes(i + 1)
-            finish(i - OUT_LAG)
             square(i + 3)
+            finish(i - OUT_LAG)
         n = n_chunks
         transposes_out(n - 5)
         quantise(n - 2)

@@ -104,7 +104,6 @@ def tile_boundedparaboloids_t_kernel(tc, x, shift, semi_axis, sharpness, multipl
         shift_inv = opool.tile([P, 2, F], F32, name="shift_inv", tag="res")
         c_terms = opool.tile([P, 2, F], F32, name="c_terms", tag="res")
         c_sum = const.tile([P, 2], F32, name="c_sum")
-        w_bf = const.tile([P, 4 * F], BF16, name="w_bf")
         w_grouped = const.tile([P, 4 * F], BF16, name="w_grouped", align_bytes=64)
         w_codes = const.tile([P, F], U32, name="w_codes", align_bytes=64)
         w_scales = const.tile([P, F], U8, name="w_scales", align_bytes=64)
@@ -139,14 +138,6 @@ def tile_boundedparaboloids_t_kernel(tc, x, shift, semi_axis, sharpness, multipl
         def shift_times_inverse(h):
             nc.vector.tensor_tensor(out=shift_inv[:, h, :], in0=shift_sb[:, h, :], in1=inv[:, h, :], op=ALU.mult)
 
-        def round_inverse(h):
-            nc.scalar.copy(out=w_bf[:, 2 * h * F : (2 * h + 1) * F], in_=inv[:, h, :])
-
-        def round_shift_inverse(h):
-            nc.scalar.activation(
-                out=w_bf[:, (2 * h + 1) * F : (2 * h + 2) * F], in_=shift_inv[:, h, :], func=ACT.Copy, scale=2.0
-            )
-
         def small_vectors():
             cols_ps = ps_o.tile([P, F], F32, name="cols_ps", tag="ot")
             for v in range(2):
@@ -157,17 +148,19 @@ def tile_boundedparaboloids_t_kernel(tc, x, shift, semi_axis, sharpness, multipl
             nc.tensor.matmul(out=mult_ps[:, 0:U], lhsT=ones_bf[:], rhs=rows_bf[:, 2 * P : 2 * P + U], start=True, stop=True)
             nc.scalar.copy(out=mult_row[:], in_=mult_ps[:, 0:U])
 
-        def weights_group(h):
-            w_words = w_bf[:].bitcast(F32)
-            g_words = w_grouped[:].bitcast(F32)
-            wt = ps_q.tile([P, 2, U], F32, name="wt", tag="q")
-            for m in range(2):
-                for u in range(2):
-                    col = 512 * h + 256 * m + P * u
-                    nc.tensor.transpose(wt[:, u, m * P : (m + 1) * P], w_words[:, col : col + P], ident[:])
-            nc.scalar.copy(
-                out=g_words[:, 512 * h : 512 * (h + 1)].rearrange("p (c u) -> p c u", u=2),
-                in_=wt[:].rearrange("p u c -> p c u"),
+        def weight_turn(values, m, h):
+            wt = (ps_q, ps_o)[m].tile([P, 4, P], F32, name="wt", tag=("q", "ot")[m])
+            for k in range(4):
+                first = (F // 2) * (k // 2) + k % 2
+                nc.tensor.transpose(wt[:, k, :], values[:, h, first : first + F // 2 - 1 : 2], ident[:])
+            return wt
+
+        def weight_round(wt, m, h):
+            nc.scalar.activation(
+                out=w_grouped[:, (2 * h + m) * F : (2 * h + m + 1) * F].rearrange("p (c k) -> p c k", k=4),
+                in_=wt[:].rearrange("p k c -> p c k"),
+                func=ACT.Copy,
+                scale=(1.0, 2.0)[m],
             )
 
         def weights_quantise(h):
@@ -221,6 +214,8 @@ def tile_boundedparaboloids_t_kernel(tc, x, shift, semi_axis, sharpness, multipl
                 load_x(j + X_BUFS)
 
         def copy_in_half(c, half):
+            if not live(c) or half >= chunk_home[c][2] // 2:
+                return
             if half == 0:
                 gg_tiles[c] = ggpool.tile([P, 8 * F], BF16, name="gg", tag="gg", align_bytes=64)
             gg_words = gg_tiles[c][:].bitcast(F32)
@@ -277,7 +272,7 @@ def tile_boundedparaboloids_t_kernel(tc, x, shift, semi_axis, sharpness, multipl
             cols = chunk_home[c][2] * P
             banks = []
             for h in range(2):
-                if c == n_chunks - 1:
+                if c >= n_chunks - 2:
                     q = ps_x.tile([P, F], F32, name="q_last", tag="xt")
                 else:
                     q = ps_q.tile([P, F], F32, name="q", tag="q")
@@ -299,24 +294,28 @@ def tile_boundedparaboloids_t_kernel(tc, x, shift, semi_axis, sharpness, multipl
         def in_tail(c):
             return c >= n_chunks - TAIL
 
-        def sigmoid(c):
+        def sigmoid_half(c, h):
             if not live(c):
                 return
             cols = chunk_home[c][2] * P
-            sig = spool.tile([P, 2, F], F32, name="sig", tag="sig")
-            for h in range(2):
-                nc.scalar.activation(
-                    out=sig[:, h, 0:cols],
-                    in_=q_banks[c][h][:, 0:cols],
-                    func=ACT.Sigmoid,
-                    scale=neg_sharp[:, h : h + 1],
-                    bias=bias[:, h : h + 1],
-                )
-            if not in_tail(c):
+            if h == 0:
+                sig_tiles[c] = spool.tile([P, 2, F], F32, name="sig", tag="sig")
+            sig = sig_tiles[c]
+            nc.scalar.activation(
+                out=sig[:, h, 0:cols],
+                in_=q_banks[c][h][:, 0:cols],
+                func=ACT.Sigmoid,
+                scale=neg_sharp[:, h : h + 1],
+                bias=bias[:, h : h + 1],
+            )
+            if h == 0 and not in_tail(c):
                 nc.gpsimd.tensor_scalar(
                     out=sig[:, 0, :], in0=sig[:, 0, :], scalar1=mult_col[:, 0:1], scalar2=0.0, op0=ALU.mult, op1=ALU.add
                 )
-            sig_tiles[c] = sig
+
+        def sigmoid(c):
+            for h in range(2):
+                sigmoid_half(c, h)
 
         def transposes_out(c):
             if not live(c):
@@ -325,10 +324,10 @@ def tile_boundedparaboloids_t_kernel(tc, x, shift, semi_axis, sharpness, multipl
             sig = sig_tiles[c]
             banks = []
             for h in range(2):
-                if c == n_chunks - 1:
-                    ot = ps_q.tile([P, CHUNK_TILES, P], F32, name="ot_last", tag="q")
+                if c in (n_chunks - 1, n_chunks - 5):
+                    ot = ps_x.tile([P, CHUNK_TILES, P], F32, name="ot_x", tag="xt")
                 elif c == n_chunks - 3:
-                    ot = ps_x.tile([P, CHUNK_TILES, P], F32, name="ot_spare", tag="xt")
+                    ot = ps_q.tile([P, CHUNK_TILES, P], F32, name="ot_q", tag="q")
                 else:
                     ot = ps_o.tile([P, CHUNK_TILES, P], F32, name="ot", tag="ot")
                 for t in range(n):
@@ -379,27 +378,29 @@ def tile_boundedparaboloids_t_kernel(tc, x, shift, semi_axis, sharpness, multipl
         inverse_check(1)
         inverse(0)
         inverse(1)
+        wt = weight_turn(inv, 0, 0)
         inverse_check(2)
         shift_times_inverse(0)
         inverse_check(3)
         inverse(2)
         inverse(3)
+        ws = weight_turn(shift_inv, 1, 0)
         copy_in_half(0, 0)
         copy_in_half(0, 1)
-        round_inverse(0)
-        round_shift_inverse(0)
+        weight_round(wt, 0, 0)
+        weight_round(ws, 1, 0)
         square_half(0, 0)
         shift_times_inverse(1)
         square_half(0, 1)
+        wt = weight_turn(inv, 0, 1)
+        ws = weight_turn(shift_inv, 1, 1)
         copy_in_half(1, 0)
-        round_inverse(1)
-        weights_group(0)
-        round_shift_inverse(1)
+        weight_round(wt, 0, 1)
+        weight_round(ws, 1, 1)
         sum_c(0)
         quantise(0)
         copy_in_half(1, 1)
         nc.scalar.activation(out=warm_out[:], in_=warm[:], func=ACT.Sigmoid)
-        weights_group(1)
         square_half(1, 0)
         weights_quantise(0)
         sum_c(1)
@@ -424,22 +425,24 @@ def tile_boundedparaboloids_t_kernel(tc, x, shift, semi_axis, sharpness, multipl
             transposes_in(i + 4)
             quantise(i + 1)
             sigmoid(i)
-            mx_passes(i + 1)
+            if i < n_chunks - 4:
+                mx_passes(i + 1)
             square(i + 3)
             finish(i - OUT_LAG)
         n = n_chunks
         transposes_out(n - 5)
+        mx_passes(n - 3)
         quantise(n - 2)
         quantise(n - 1)
-        sigmoid(n - 3)
-        mx_passes(n - 2)
         finish(n - 5)
+        sigmoid(n - 3)
         transposes_out(n - 4)
-        sigmoid(n - 2)
+        mx_passes(n - 2)
         mx_passes(n - 1)
         finish(n - 4)
-        transposes_out(n - 3)
+        sigmoid(n - 2)
         sigmoid(n - 1)
+        transposes_out(n - 3)
         transposes_out(n - 2)
         finish(n - 3)
         transposes_out(n - 1)

@@ -23,6 +23,7 @@ O_BUFS = 26
 GPSIMD_ROWS = 64
 FIRST_GPSIMD_CHUNK = 5
 PIECES = 2
+VECTOR_COPIES = ((0, 0),)
 OUT_LAG = 2
 TAIL = 2
 
@@ -98,8 +99,6 @@ def tile_boundedparaboloids_t_kernel(tc, x, shift, semi_axis, sharpness, multipl
 
         neg_semi_sq = opool.tile([P, 2, F], F32, name="neg_semi_sq", tag="res")
         root = opool.tile([P, 2, F], F32, name="root", tag="res")
-        guess = opool.tile([P, 2, F], F32, name="guess", tag="res")
-        check = opool.tile([P, 2, F], F32, name="check", tag="res")
         inv = opool.tile([P, 2, F], F32, name="inv", tag="res")
         shift_inv = opool.tile([P, 2, F], F32, name="shift_inv", tag="res")
         c_terms = opool.tile([P, 2, F], F32, name="c_terms", tag="res")
@@ -124,16 +123,8 @@ def tile_boundedparaboloids_t_kernel(tc, x, shift, semi_axis, sharpness, multipl
         def inverse_root(i):
             nc.scalar.activation(out=piece(root, i), in_=piece(neg_semi_sq, i), func=ACT.Abs_reciprocal_sqrt)
 
-        def inverse_guess(i):
-            nc.scalar.activation(out=piece(guess, i), in_=piece(root, i), func=ACT.Square)
-
-        def inverse_check(i):
-            nc.vector.tensor_tensor(out=piece(check, i), in0=piece(neg_semi_sq, i), in1=piece(guess, i), op=ALU.mult)
-
         def inverse(i):
-            nc.vector.scalar_tensor_tensor(
-                out=piece(inv, i), in0=piece(check, i), scalar=2.0, in1=piece(guess, i), op0=ALU.add, op1=ALU.mult
-            )
+            nc.scalar.activation(out=piece(inv, i), in_=piece(root, i), func=ACT.Square)
 
         def shift_times_inverse(h):
             nc.vector.tensor_tensor(out=shift_inv[:, h, :], in0=shift_sb[:, h, :], in1=inv[:, h, :], op=ALU.mult)
@@ -219,7 +210,8 @@ def tile_boundedparaboloids_t_kernel(tc, x, shift, semi_axis, sharpness, multipl
             if half == 0:
                 gg_tiles[c] = ggpool.tile([P, 8 * F], BF16, name="gg", tag="gg", align_bytes=64)
             gg_words = gg_tiles[c][:].bitcast(F32)
-            nc.scalar.copy(
+            move = nc.vector.tensor_copy if (c, half) in VECTOR_COPIES else nc.scalar.copy
+            move(
                 out=gg_words[:, 512 * half : 512 * (half + 1)].rearrange("p (c u) -> p c u", u=2),
                 in_=xt_banks[c][half][:].rearrange("p u c -> p c u"),
             )
@@ -365,57 +357,48 @@ def tile_boundedparaboloids_t_kernel(tc, x, shift, semi_axis, sharpness, multipl
         negative_square(3)
         nc.gpsimd.tensor_scalar(out=rows_f32[:], in0=rows_bf[:, 0 : 2 * P], scalar1=1.0, scalar2=0.0, op0=ALU.mult, op1=ALU.add)
         transposes_in(0)
-        transposes_in(1)
         inverse_root(0)
         inverse_root(1)
-        inverse_guess(0)
-        inverse_guess(1)
-        inverse_root(2)
-        inverse_root(3)
-        inverse_guess(2)
-        inverse_guess(3)
-        inverse_check(0)
-        inverse_check(1)
         inverse(0)
         inverse(1)
-        wt = weight_turn(inv, 0, 0)
-        inverse_check(2)
-        shift_times_inverse(0)
-        inverse_check(3)
+        inverse_root(2)
+        inverse_root(3)
         inverse(2)
         inverse(3)
-        ws = weight_turn(shift_inv, 1, 0)
+        wt = weight_turn(inv, 0, 0)
         copy_in_half(0, 0)
-        copy_in_half(0, 1)
+        shift_times_inverse(0)
+        ws = weight_turn(shift_inv, 1, 0)
+        transposes_in(1)
         weight_round(wt, 0, 0)
-        weight_round(ws, 1, 0)
+        copy_in_half(0, 1)
         square_half(0, 0)
         shift_times_inverse(1)
         square_half(0, 1)
+        weight_round(ws, 1, 0)
         wt = weight_turn(inv, 0, 1)
         ws = weight_turn(shift_inv, 1, 1)
         copy_in_half(1, 0)
         weight_round(wt, 0, 1)
         weight_round(ws, 1, 1)
-        sum_c(0)
-        quantise(0)
-        copy_in_half(1, 1)
-        nc.scalar.activation(out=warm_out[:], in_=warm[:], func=ACT.Sigmoid)
-        square_half(1, 0)
-        weights_quantise(0)
-        sum_c(1)
-        square_half(1, 1)
-        weights_quantise(1)
         transposes_in(2)
+        copy_in_half(1, 1)
+        quantise(0)
+        weights_quantise(0)
+        copy_in(2)
+        sum_c(0)
+        weights_quantise(1)
+        sum_c(1)
         small_vectors()
         mx_passes(0)
-        transposes_in(3)
-        copy_in(2)
+        nc.scalar.activation(out=warm_out[:], in_=warm[:], func=ACT.Sigmoid)
         sigmoid_bias()
+        square(1)
+        transposes_in(3)
         quantise(1)
-        square(2)
         sigmoid(0)
         copy_in(3)
+        square(2)
         transposes_in(4)
         mx_passes(1)
         square(3)

@@ -17,7 +17,7 @@ FLOPS = 2 * 2 * B * U * F
 
 ROW_TILES = B // P
 CHUNK_TILES = 4
-LOADS = [[4], [4]] + [[4, 4]] * 14 + [[4, 2, 2]]
+LOADS = [[4]] * 4 + [[4, 4]] * 13 + [[4, 2, 2]]
 X_BUFS = 5
 O_BUFS = 26
 GPSIMD_ROWS = 64
@@ -73,18 +73,18 @@ def tile_boundedparaboloids_t_kernel(tc, x, shift, semi_axis, sharpness, multipl
                 nc.sync.dma_start(out=xt[:, i * width : (i + 1) * width], in_=rows[:, i * width : (i + 1) * width])
             x_tiles[j] = xt
 
+        rows_bf = const.tile([P, 2 * P + U], BF16, name="rows_bf")
+        nc.vector.memset(rows_bf[:], 0.0)
         semi_sb = const.tile([P, 2, F], BF16, name="semi_sb")
         for h in range(2):
             nc.sync.dma_start(out=semi_sb[:, h, :], in_=semi_axis[h * P : (h + 1) * P, :])
         load_x(0, pieces=2)
-        shift_sb = const.tile([P, 2, F], BF16, name="shift_sb")
-        nc.sync.dma_start(out=shift_sb[:], in_=shift.rearrange("(h p f) -> p h f", h=2, p=P))
-        load_x(1)
-        rows_bf = const.tile([P, 2 * P + U], BF16, name="rows_bf")
-        nc.vector.memset(rows_bf[:], 0.0)
         nc.sync.dma_start(out=rows_bf[0:2, 0:P], in_=sharpness.rearrange("(h p) -> h p", h=2))
         nc.sync.dma_start(out=rows_bf[0:2, P : 2 * P], in_=multiplier.rearrange("(h p) -> h p", h=2))
         nc.sync.dma_start(out=rows_bf[0:1, 2 * P : 2 * P + U], in_=multiplier.rearrange("(o u) -> o u", o=1))
+        shift_sb = const.tile([P, 2, F], BF16, name="shift_sb")
+        nc.sync.dma_start(out=shift_sb[:], in_=shift.rearrange("(h p f) -> p h f", h=2, p=P))
+        load_x(1)
         for j in range(2, X_BUFS):
             load_x(j)
 
@@ -381,24 +381,26 @@ def tile_boundedparaboloids_t_kernel(tc, x, shift, semi_axis, sharpness, multipl
         copy_in_half(1, 0)
         weight_round(wt, 0, 1)
         weight_round(ws, 1, 1)
-        transposes_in(2)
-        copy_in_half(1, 1)
+        sum_c(0)
         quantise(0)
         weights_quantise(0)
-        copy_in(2)
-        sum_c(0)
-        weights_quantise(1)
         sum_c(1)
+        weights_quantise(1)
+        transposes_in(2)
+        copy_in_half(1, 1)
+        square_half(1, 0)
         small_vectors()
+        sigmoid_bias()
+        square_half(1, 1)
+        copy_in(2)
         mx_passes(0)
         nc.scalar.activation(out=warm_out[:], in_=warm[:], func=ACT.Sigmoid)
-        sigmoid_bias()
-        square(1)
-        transposes_in(3)
+        square_half(2, 0)
         quantise(1)
+        square_half(2, 1)
+        transposes_in(3)
         sigmoid(0)
         copy_in(3)
-        square(2)
         transposes_in(4)
         mx_passes(1)
         square(3)
@@ -415,17 +417,17 @@ def tile_boundedparaboloids_t_kernel(tc, x, shift, semi_axis, sharpness, multipl
         n = n_chunks
         transposes_out(n - 5)
         mx_passes(n - 3)
+        finish(n - 5)
         quantise(n - 2)
         quantise(n - 1)
-        finish(n - 5)
         sigmoid(n - 3)
         transposes_out(n - 4)
+        finish(n - 4)
         mx_passes(n - 2)
         mx_passes(n - 1)
-        finish(n - 4)
         sigmoid(n - 2)
-        sigmoid(n - 1)
         transposes_out(n - 3)
+        sigmoid(n - 1)
         transposes_out(n - 2)
         finish(n - 3)
         transposes_out(n - 1)

@@ -417,19 +417,19 @@ def tile_boundedparaboloids_t_kernel(tc, x, shift, semi_axis, sharpness, multipl
         n = n_chunks
         transposes_out(n - 5)
         mx_passes(n - 3)
-        finish(n - 5)
         quantise(n - 2)
-        quantise(n - 1)
+        finish(n - 5)
         sigmoid(n - 3)
         transposes_out(n - 4)
-        finish(n - 4)
         mx_passes(n - 2)
-        mx_passes(n - 1)
+        finish(n - 4)
+        quantise(n - 1)
         sigmoid(n - 2)
         transposes_out(n - 3)
+        mx_passes(n - 1)
+        finish(n - 3)
         sigmoid(n - 1)
         transposes_out(n - 2)
-        finish(n - 3)
         transposes_out(n - 1)
         finish(n - 2)
         finish(n - 1)

from contextlib import ExitStack

import concourse.mybir as mybir
from concourse.masks import make_identity

F32 = mybir.dt.float32
BF16 = mybir.dt.bfloat16
U32 = mybir.dt.uint32
U8 = mybir.dt.uint8
FP8X4 = mybir.dt.float8_e4m3fn_x4
ACT = mybir.ActivationFunctionType
ALU = mybir.AluOpType

P = 128
B, U, F = 16384, 256, 512
FLOPS = 2 * 2 * B * U * F

ROW_TILES = B // P
CHUNK_TILES = 4
LOADS = [[4]] * 4 + [[4, 4]] * 13 + [[4, 2, 2]]
X_BUFS = 5
O_BUFS = 26
GPSIMD_ROWS = 64
FIRST_GPSIMD_CHUNK = 5
PIECES = 2
VECTOR_COPIES = ((0, 0),)
OUT_LAG = 2
TAIL = 2


def tile_boundedparaboloids_t_kernel(tc, x, shift, semi_axis, sharpness, multiplier, out):
    nc = tc.nc
    assert sum(sum(chunks) for chunks in LOADS) == ROW_TILES
    with ExitStack() as ctx:
        const = ctx.enter_context(tc.tile_pool(name="const", bufs=1))
        xpool = ctx.enter_context(tc.tile_pool(name="xpool", bufs=X_BUFS))
        ggpool = ctx.enter_context(tc.tile_pool(name="ggpool", bufs=4))
        cpool = ctx.enter_context(tc.tile_pool(name="cpool", bufs=4))
        spool = ctx.enter_context(tc.tile_pool(name="spool", bufs=4))
        opool = ctx.enter_context(tc.tile_pool(name="opool", bufs=O_BUFS))
        ps_x = ctx.enter_context(tc.psum_pool(name="ps_x", bufs=4))
        ps_q = ctx.enter_context(tc.psum_pool(name="ps_q", bufs=2))
        ps_o = ctx.enter_context(tc.psum_pool(name="ps_o", bufs=2))
        ctx.enter_context(tc.manual_schedule())

        load_base = []
        load_tiles = []
        chunk_home = []
        base = 0
        for j, chunks in enumerate(LOADS):
            load_base.append(base)
            load_tiles.append(sum(chunks))
            t0 = 0
            for n in chunks:
                chunk_home.append((j, t0, n))
                t0 += n
            base += t0 * P
        n_chunks = len(chunk_home)
        last_chunk_of_load = {}
        for c, (j, t0, n) in enumerate(chunk_home):
            last_chunk_of_load[j] = c

        x_tiles = {}

        def load_x(j, pieces=1):
            if j >= len(LOADS):
                return
            t_count = load_tiles[j]
            xt = xpool.tile([P, 8 * F], BF16, name="x_sb", tag="x_sb")
            rows = x[load_base[j] : load_base[j] + t_count * P, :].rearrange("(p t) f -> p (t f)", t=t_count)
            width = t_count * F // pieces
            for i in range(pieces):
                nc.sync.dma_start(out=xt[:, i * width : (i + 1) * width], in_=rows[:, i * width : (i + 1) * width])
            x_tiles[j] = xt

        rows_bf = const.tile([P, 2 * P + U], BF16, name="rows_bf")
        nc.vector.memset(rows_bf[:], 0.0)
        semi_sb = const.tile([P, 2, F], BF16, name="semi_sb")
        for h in range(2):
            nc.sync.dma_start(out=semi_sb[:, h, :], in_=semi_axis[h * P : (h + 1) * P, :])
        load_x(0, pieces=2)
        nc.sync.dma_start(out=rows_bf[0:2, 0:P], in_=sharpness.rearrange("(h p) -> h p", h=2))
        nc.sync.dma_start(out=rows_bf[0:2, P : 2 * P], in_=multiplier.rearrange("(h p) -> h p", h=2))
        nc.sync.dma_start(out=rows_bf[0:1, 2 * P : 2 * P + U], in_=multiplier.rearrange("(o u) -> o u", o=1))
        shift_sb = const.tile([P, 2, F], BF16, name="shift_sb")
        nc.sync.dma_start(out=shift_sb[:], in_=shift.rearrange("(h p f) -> p h f", h=2, p=P))
        load_x(1)
        for j in range(2, X_BUFS):
            load_x(j)

        ident = const.tile([P, P], F32, name="ident")
        make_identity(nc, ident[:])
        ones_bf = const.tile([P, P], BF16, name="ones_bf")
        nc.vector.memset(ones_bf[:], 1.0)
        warm = const.tile([P, 1], F32, name="warm")
        nc.vector.memset(warm[:], 1.0)
        warm_out = const.tile([P, 1], F32, name="warm_out")
        nc.scalar.activation(out=warm_out[:], in_=warm[:], func=ACT.Abs_reciprocal_sqrt)

        neg_semi_sq = opool.tile([P, 2, F], F32, name="neg_semi_sq", tag="res")
        root = opool.tile([P, 2, F], F32, name="root", tag="res")
        inv = opool.tile([P, 2, F], F32, name="inv", tag="res")
        shift_inv = opool.tile([P, 2, F], F32, name="shift_inv", tag="res")
        c_terms = opool.tile([P, 2, F], F32, name="c_terms", tag="res")
        c_sum = const.tile([P, 2], F32, name="c_sum")
        w_grouped = const.tile([P, 4 * F], BF16, name="w_grouped", align_bytes=64)
        w_codes = const.tile([P, F], U32, name="w_codes", align_bytes=64)
        w_scales = const.tile([P, F], U8, name="w_scales", align_bytes=64)
        rows_f32 = const.tile([P, 2 * P], F32, name="rows_f32")
        neg_sharp = const.tile([P, 2], F32, name="neg_sharp")
        bias = const.tile([P, 2], F32, name="bias")
        mult_col = const.tile([P, 1], F32, name="mult_col")
        mult_row = const.tile([P, U], F32, name="mult_row")

        def piece(tile, i):
            return tile[:, i // PIECES, i % PIECES * (F // PIECES) : (i % PIECES + 1) * (F // PIECES)]

        def negative_square(i):
            nc.vector.scalar_tensor_tensor(
                out=piece(neg_semi_sq, i), in0=piece(semi_sb, i), scalar=-1.0, in1=piece(semi_sb, i), op0=ALU.mult, op1=ALU.mult
            )

        def inverse_root(i):
            nc.scalar.activation(out=piece(root, i), in_=piece(neg_semi_sq, i), func=ACT.Abs_reciprocal_sqrt)

        def inverse(i):
            nc.scalar.activation(out=piece(inv, i), in_=piece(root, i), func=ACT.Square)

        def shift_times_inverse(h):
            nc.vector.tensor_tensor(out=shift_inv[:, h, :], in0=shift_sb[:, h, :], in1=inv[:, h, :], op=ALU.mult)

        def small_vectors():
            cols_ps = ps_o.tile([P, F], F32, name="cols_ps", tag="ot")
            for v in range(2):
                nc.tensor.transpose(cols_ps[:, v * P : (v + 1) * P], rows_f32[:, v * P : (v + 1) * P], ident[:])
            nc.scalar.activation(out=neg_sharp[:], in_=cols_ps[:, 0:2], func=ACT.Copy, scale=-1.0)
            nc.scalar.copy(out=mult_col[:], in_=cols_ps[:, P : P + 1])
            mult_ps = ps_o.tile([P, F], F32, name="mult_ps", tag="ot")
            nc.tensor.matmul(out=mult_ps[:, 0:U], lhsT=ones_bf[:], rhs=rows_bf[:, 2 * P : 2 * P + U], start=True, stop=True)
            nc.scalar.copy(out=mult_row[:], in_=mult_ps[:, 0:U])

        def weight_turn(values, m, h):
            wt = (ps_q, ps_o)[m].tile([P, 4, P], F32, name="wt", tag=("q", "ot")[m])
            for k in range(4):
                first = (F // 2) * (k // 2) + k % 2
                nc.tensor.transpose(wt[:, k, :], values[:, h, first : first + F // 2 - 1 : 2], ident[:])
            return wt

        def weight_round(wt, m, h):
            nc.scalar.activation(
                out=w_grouped[:, (2 * h + m) * F : (2 * h + m + 1) * F].rearrange("p (c k) -> p c k", k=4),
                in_=wt[:].rearrange("p k c -> p c k"),
                func=ACT.Copy,
                scale=(1.0, 2.0)[m],
            )

        def weights_quantise(h):
            nc.vector.quantize_mx(
                out=w_codes[:, U * h : U * (h + 1)].bitcast(FP8X4),
                scales=w_scales[:, U * h : U * (h + 1)],
                in_=w_grouped[:, 2 * F * h : 2 * F * (h + 1)],
            )

        def sum_c(h):
            nc.vector.scalar_tensor_tensor(
                out=c_terms[:, h, :],
                in0=shift_inv[:, h, :],
                scalar=1.0,
                in1=shift_sb[:, h, :],
                op0=ALU.mult,
                op1=ALU.mult,
                accum_out=c_sum[:, h : h + 1],
            )

        def sigmoid_bias():
            nc.vector.scalar_tensor_tensor(
                out=bias[:], in0=c_sum[:], scalar=-1.0, in1=neg_sharp[:], op0=ALU.add, op1=ALU.mult
            )

        xt_banks = {}
        gg_tiles = {}
        code_tiles = {}
        q_banks = {}
        sig_tiles = {}
        ot_banks = {}

        def live(c):
            return 0 <= c < n_chunks

        def transposes_in(c):
            if not live(c):
                return
            j, t0, n = chunk_home[c]
            words = x_tiles[j][:].bitcast(F32)
            banks = []
            for half in range(n // 2):
                xt = ps_x.tile([P, 2, 2 * P], F32, name="xt", tag="xt")
                for tt in range(2):
                    for u in range(2):
                        col = (t0 + 2 * half + tt) * (F // 2) + P * u
                        nc.tensor.transpose(xt[:, u, tt * P : (tt + 1) * P], words[:, col : col + P], ident[:])
                banks.append(xt)
            xt_banks[c] = banks
            if last_chunk_of_load[j] == c:
                load_x(j + X_BUFS)

        def copy_in_half(c, half):
            if not live(c) or half >= chunk_home[c][2] // 2:
                return
            if half == 0:
                gg_tiles[c] = ggpool.tile([P, 8 * F], BF16, name="gg", tag="gg", align_bytes=64)
            gg_words = gg_tiles[c][:].bitcast(F32)
            move = nc.vector.tensor_copy if (c, half) in VECTOR_COPIES else nc.scalar.copy
            move(
                out=gg_words[:, 512 * half : 512 * (half + 1)].rearrange("p (c u) -> p c u", u=2),
                in_=xt_banks[c][half][:].rearrange("p u c -> p c u"),
            )

        def square_half(c, half):
            gg = gg_tiles[c]
            n = chunk_home[c][2]
            rows = 2 * P
            if n == CHUNK_TILES and half == 0 and c >= FIRST_GPSIMD_CHUNK:
                rows -= GPSIMD_ROWS
                x_cols = slice(4 * rows, 2 * F)
                sq_cols = slice(n * F + 4 * rows, n * F + 2 * F)
                nc.gpsimd.tensor_tensor(out=gg[:, sq_cols], in0=gg[:, x_cols], in1=gg[:, x_cols], op=ALU.mult)
            x_cols = slice(2 * F * half, 2 * F * half + 4 * rows)
            sq_cols = slice(n * F + 2 * F * half, n * F + 2 * F * half + 4 * rows)
            nc.vector.tensor_tensor(
                out=gg[:, sq_cols].rearrange("p (c u e) -> p c u e", u=2, e=2),
                in0=xt_banks[c][half][:].bitcast(BF16).rearrange("p u (c e) -> p c u e", e=2)[:, 0:rows],
                in1=gg[:, x_cols].rearrange("p (c u e) -> p c u e", u=2, e=2),
                op=ALU.mult,
            )

        def copy_in(c):
            if not live(c):
                return
            for half in range(chunk_home[c][2] // 2):
                copy_in_half(c, half)

        def square(c):
            if not live(c):
                return
            for half in range(chunk_home[c][2] // 2):
                square_half(c, half)

        def quantise(c):
            if not live(c):
                return
            n = chunk_home[c][2]
            codes = cpool.tile([P, 2 * F], U32, name="codes", tag="codes", align_bytes=64)
            scales = cpool.tile([P, 2 * F], U8, name="scales", tag="scales", align_bytes=64)
            nc.vector.quantize_mx(
                out=codes[:, 0 : 2 * n * P].bitcast(FP8X4), scales=scales[:, 0 : 2 * n * P], in_=gg_tiles[c][:, 0 : 2 * n * F]
            )
            code_tiles[c] = (codes, scales)

        def mx_passes(c):
            if not live(c):
                return
            codes, scales = code_tiles[c]
            cols = chunk_home[c][2] * P
            banks = []
            for h in range(2):
                if c >= n_chunks - 2:
                    q = ps_x.tile([P, F], F32, name="q_last", tag="xt")
                else:
                    q = ps_q.tile([P, F], F32, name="q", tag="q")
                for m in range(2):
                    w_cols = slice(U * h + P * m, U * h + P * (m + 1))
                    x_cols = slice(cols * (1 - m), cols * (2 - m))
                    nc.tensor.matmul_mx(
                        out=q[:, 0:cols],
                        lhsT=w_codes[:, w_cols].bitcast(FP8X4),
                        lhsT_scale=w_scales[:, w_cols],
                        rhs=codes[:, x_cols].bitcast(FP8X4),
                        rhs_scale=scales[:, x_cols],
                        start=(m == 0),
                        stop=(m == 1),
                    )
                banks.append(q)
            q_banks[c] = banks

        def in_tail(c):
            return c >= n_chunks - TAIL

        def sigmoid_half(c, h):
            if not live(c):
                return
            cols = chunk_home[c][2] * P
            if h == 0:
                sig_tiles[c] = spool.tile([P, 2, F], F32, name="sig", tag="sig")
            sig = sig_tiles[c]
            nc.scalar.activation(
                out=sig[:, h, 0:cols],
                in_=q_banks[c][h][:, 0:cols],
                func=ACT.Sigmoid,
                scale=neg_sharp[:, h : h + 1],
                bias=bias[:, h : h + 1],
            )
            if h == 0 and not in_tail(c):
                nc.gpsimd.tensor_scalar(
                    out=sig[:, 0, :], in0=sig[:, 0, :], scalar1=mult_col[:, 0:1], scalar2=0.0, op0=ALU.mult, op1=ALU.add
                )

        def sigmoid(c):
            for h in range(2):
                sigmoid_half(c, h)

        def transposes_out(c):
            if not live(c):
                return
            n = chunk_home[c][2]
            sig = sig_tiles[c]
            banks = []
            for h in range(2):
                if c in (n_chunks - 1, n_chunks - 5):
                    ot = ps_x.tile([P, CHUNK_TILES, P], F32, name="ot_x", tag="xt")
                elif c == n_chunks - 3:
                    ot = ps_q.tile([P, CHUNK_TILES, P], F32, name="ot_q", tag="q")
                else:
                    ot = ps_o.tile([P, CHUNK_TILES, P], F32, name="ot", tag="ot")
                for t in range(n):
                    nc.tensor.transpose(ot[:, t, :], sig[:, h, t * P : (t + 1) * P], ident[:])
                banks.append(ot)
            ot_banks[c] = banks

        def multiply_out(c, res, h):
            n = chunk_home[c][2]
            units = slice(h * P, (h + 1) * P)
            nc.vector.tensor_tensor(
                out=res[:, 0:n, units],
                in0=ot_banks[c][h][:, 0:n, :],
                in1=mult_row[:, units].unsqueeze(1).to_broadcast([P, n, P]),
                op=ALU.mult,
            )

        def finish(c):
            if not live(c):
                return
            j, t0, n = chunk_home[c]
            t_count = load_tiles[j]
            res = opool.tile([P, CHUNK_TILES, U], F32, name="res", tag="res")
            if in_tail(c):
                multiply_out(c, res, 0)
            else:
                nc.scalar.copy(out=res[:, :, 0:P], in_=ot_banks[c][0][:])
            multiply_out(c, res, 1)
            rows = out[load_base[j] : load_base[j] + t_count * P, :].rearrange("(p t) u -> p (t u)", t=t_count)
            nc.sync.dma_start(out=rows[:, t0 * U : (t0 + n) * U], in_=res[:, 0:n, :].rearrange("p t u -> p (t u)"))

        negative_square(0)
        negative_square(1)
        negative_square(2)
        negative_square(3)
        nc.gpsimd.tensor_scalar(out=rows_f32[:], in0=rows_bf[:, 0 : 2 * P], scalar1=1.0, scalar2=0.0, op0=ALU.mult, op1=ALU.add)
        transposes_in(0)
        inverse_root(0)
        inverse_root(1)
        inverse(0)
        inverse(1)
        inverse_root(2)
        inverse_root(3)
        inverse(2)
        inverse(3)
        wt = weight_turn(inv, 0, 0)
        copy_in_half(0, 0)
        shift_times_inverse(0)
        ws = weight_turn(shift_inv, 1, 0)
        transposes_in(1)
        weight_round(wt, 0, 0)
        copy_in_half(0, 1)
        square_half(0, 0)
        shift_times_inverse(1)
        square_half(0, 1)
        weight_round(ws, 1, 0)
        wt = weight_turn(inv, 0, 1)
        ws = weight_turn(shift_inv, 1, 1)
        copy_in_half(1, 0)
        weight_round(wt, 0, 1)
        weight_round(ws, 1, 1)
        sum_c(0)
        quantise(0)
        weights_quantise(0)
        sum_c(1)
        weights_quantise(1)
        transposes_in(2)
        copy_in_half(1, 1)
        square_half(1, 0)
        small_vectors()
        sigmoid_bias()
        square_half(1, 1)
        copy_in(2)
        mx_passes(0)
        nc.scalar.activation(out=warm_out[:], in_=warm[:], func=ACT.Sigmoid)
        square_half(2, 0)
        quantise(1)
        square_half(2, 1)
        transposes_in(3)
        sigmoid(0)
        copy_in(3)
        transposes_in(4)
        mx_passes(1)
        square(3)
        for i in range(1, n_chunks - 3):
            transposes_out(i - OUT_LAG)
            copy_in(i + 3)
            transposes_in(i + 4)
            quantise(i + 1)
            sigmoid(i)
            if i < n_chunks - 4:
                mx_passes(i + 1)
            square(i + 3)
            finish(i - OUT_LAG)
        n = n_chunks
        transposes_out(n - 5)
        mx_passes(n - 3)
        quantise(n - 2)
        finish(n - 5)
        sigmoid(n - 3)
        transposes_out(n - 4)
        mx_passes(n - 2)
        finish(n - 4)
        quantise(n - 1)
        sigmoid(n - 2)
        transposes_out(n - 3)
        mx_passes(n - 1)
        finish(n - 3)
        sigmoid(n - 1)
        transposes_out(n - 2)
        transposes_out(n - 1)
        finish(n - 2)
        finish(n - 1)
